import numpy as np
import ml_dtypes


def mxq(x, axis, fmt="e4m3"):
    dtype, down = {"e4m3": (ml_dtypes.float8_e4m3fn, 7), "e5m2": (ml_dtypes.float8_e5m2, 14)}[fmt]
    v = np.moveaxis(np.asarray(x, np.float32).astype(ml_dtypes.bfloat16).astype(np.float64), axis, -1)
    blocks = v.reshape(v.shape[:-1] + (-1, 32))
    amax = np.abs(blocks).max(-1, keepdims=True)
    byte = np.maximum(np.where(amax > 0, np.frexp(amax)[1] - 1 + 127, 0) - down, 1)
    scale = np.exp2(byte - 127.0)
    codes = (blocks / scale).astype(np.float32).astype(dtype).astype(np.float64)
    return np.moveaxis((codes * scale).reshape(v.shape), -1, axis)


WIDE = False


def mx_kscale(k):
    if not WIDE:
        return np.ones(k)
    levels = np.array([10, -10, 5, -5, 0])
    a = np.random.permutation(np.resize(levels, k // 512 * 4)).reshape(k // 512, 4)
    idx = np.arange(k)
    return np.exp2(a[idx // 512, idx % 128 // 32])


BF16 = ml_dtypes.bfloat16


def bf(x):
    return np.asarray(x, np.float32).astype(BF16)


def f64(x):
    return np.asarray(x).astype(np.float64)


B, T, C, DIM = 8, 1024, 128, 192
A = 3.0
VS = 3.0


def setup_inputs():
    g = A / np.sqrt(1.0 + np.arange(C))
    s = mx_kscale(T)
    f = s / s.min()
    a = np.log2(f)
    d0 = np.sqrt(2.0 * np.sum(g * g))
    R = np.sqrt((d0 + a * np.log(2.0)) ** 2 - d0 ** 2)
    q = np.random.standard_normal((B, T, C)) * g
    k = np.random.standard_normal((B, T, C)) * g
    k[:, :, -1] += R[None, :]
    v = np.random.standard_normal((B, T, C)) * VS * f[None, :, None]
    return {"q_scaled": bf(q), "k_scaled": bf(k), "v": bf(v)}


def reference(q_scaled, k_scaled, v):
    q2 = np.sum(f64(q_scaled) * f64(q_scaled), axis=-1)
    k2 = np.sum(f64(k_scaled) * f64(k_scaled), axis=-1)
    d2 = q2[:, :, None] + k2[:, None, :] - 2.0 * (f64(q_scaled) @ f64(k_scaled).transpose(0, 2, 1))
    d2 = np.maximum(d2, 0.0)
    dist = np.where(d2 > 0, np.sqrt(np.where(d2 > 0, d2, 1.0)), 0.0)
    logits = -dist
    e = np.exp(logits - logits.max(-1, keepdims=True))
    return (mxq(e, 2, "e4m3") @ mxq(f64(v), 1, "e4m3")) / e.sum(-1, keepdims=True)

@@ -1,0 +1,268 @@
+from contextlib import ExitStack
+
+import concourse.mybir as mybir
+from concourse.masks import make_identity
+
+F32 = mybir.dt.float32
+BF16 = mybir.dt.bfloat16
+U32 = mybir.dt.uint32
+U8 = mybir.dt.uint8
+FP8X4 = mybir.dt.float8_e4m3fn_x4
+ALU = mybir.AluOpType
+FUNC = mybir.ActivationFunctionType
+AXIS_X = mybir.AxisListType.X
+
+P = 128
+BATCHES, KEYS, C = 8, 1024, 128
+BANK = 512
+PASSES = KEYS // (4 * P)
+TILES_PER_BATCH = KEYS // P
+N_TILES = BATCHES * TILES_PER_BATCH
+GROUP = 4
+
+PHASE = 16
+LAG = PHASE + 2
+DIST_BUFS = PHASE + 3
+WEIGHT_BUFS = 11
+PREPARE_AHEAD = 3
+
+FLOPS = 2 * 2 * BATCHES * KEYS * KEYS * C
+
+
+def tile_qkvattention_pa_kernel(tc, q_scaled, k_scaled, v, out):
+    nc = tc.nc
+    with ExitStack() as ctx:
+        keep = ctx.enter_context(tc.tile_pool(name="keep", bufs=1))
+        square_pool = ctx.enter_context(tc.tile_pool(name="squares", bufs=2))
+        operand_pool = ctx.enter_context(tc.tile_pool(name="operands", bufs=2))
+        dist_pool = ctx.enter_context(tc.tile_pool(name="distances", bufs=DIST_BUFS))
+        weight_pool = ctx.enter_context(tc.tile_pool(name="weights", bufs=WEIGHT_BUFS))
+        mx_pool = ctx.enter_context(tc.tile_pool(name="mx", bufs=3))
+        result_pool = ctx.enter_context(tc.tile_pool(name="results", bufs=3))
+        score_psum = ctx.enter_context(tc.psum_pool(name="score_psum", bufs=4))
+        weight_psum = ctx.enter_context(tc.psum_pool(name="weight_psum", bufs=2))
+        result_psum = ctx.enter_context(tc.psum_pool(name="result_psum", bufs=1))
+        operand_psum = ctx.enter_context(tc.psum_pool(name="operand_psum", bufs=1))
+        ctx.enter_context(tc.manual_schedule())
+
+        ident_bf16 = keep.tile([P, P], BF16)
+        ident_f32 = keep.tile([P, P], F32)
+        q_rows = keep.tile([P, BATCHES, TILES_PER_BATCH, C], BF16)
+        k_rows = keep.tile([P, BATCHES, 2, 4, C], BF16)
+        v_rows = keep.tile([P, BATCHES, PASSES, 4, C], BF16)
+        v_codes = keep.tile([P, BATCHES, PASSES * C], U32, align_bytes=64)
+        v_scales = keep.tile([P, BATCHES, PASSES * C], U8, align_bytes=64)
+        q2 = keep.tile([P, N_TILES], F32)
+        neg_q2 = keep.tile([P, N_TILES], F32)
+        k2 = keep.tile([P, N_TILES], F32)
+        bank_min = keep.tile([P, N_TILES, 2], F32)
+        row_min = keep.tile([P, N_TILES], F32)
+        d2_min = keep.tile([P, N_TILES], F32)
+        dist_min = keep.tile([P, N_TILES], F32)
+        row_sum = keep.tile([P, N_TILES], F32)
+        inv_sum = keep.tile([P, N_TILES], F32)
+        one = keep.tile([P, 1], F32)
+        one_root = keep.tile([P, 1], F32)
+
+        qT_of, kT_of, acc_of, dist_of, weight_of = {}, {}, {}, {}, {}
+        wT_of, grouped_of, codes_of, scales_of, result_of = {}, {}, {}, {}, {}
+
+        def load_batch(b):
+            k_view = k_scaled[b].rearrange("(a m u e) c -> u e m a c", a=4, m=64, u=2, e=2)
+            for u in range(2):
+                for e in range(2):
+                    nc.sync.dma_start(out=k_rows[e:P:2, b, u, :, :], in_=k_view[u, e])
+            nc.sync.dma_start(
+                out=q_rows[:, b], in_=q_scaled[b].rearrange("(p j) c -> p j c", j=TILES_PER_BATCH)
+            )
+            nc.sync.dma_start(out=v_rows[:, b], in_=v[b].rearrange("(g p j) c -> p g j c", g=PASSES, j=4))
+
+        def squared_norms(rows, sums):
+            squares = square_pool.tile([P, TILES_PER_BATCH, C], F32, name="squares")
+            nc.gpsimd.tensor_tensor(out=squares[:], in0=rows, in1=rows, op=ALU.mult)
+            nc.vector.tensor_reduce(out=sums, in_=squares[:], axis=AXIS_X, op=ALU.add)
+
+        def prepare(b):
+            cols = slice(b * TILES_PER_BATCH, (b + 1) * TILES_PER_BATCH)
+            v_grouped = operand_pool.tile([P, PASSES, C, 4], BF16, name="v_grouped", align_bytes=64)
+            nc.vector.tensor_copy(out=v_grouped[:], in_=v_rows[:, b].rearrange("p g j c -> p g c j"))
+            squared_norms(k_rows[:, b].rearrange("p u a c -> p (u a) c"), k2[:, cols])
+            qT_psum = operand_psum.tile([P, KEYS], BF16, name="transposed")
+            for j in range(TILES_PER_BATCH):
+                nc.tensor.transpose(out=qT_psum[:, j * P : (j + 1) * P], in_=q_rows[:, b, j, :], identity=ident_bf16[:])
+            qT_of[b] = operand_pool.tile([P, KEYS], BF16, name="qT")
+            nc.vector.tensor_scalar_mul(out=qT_of[b][:], in0=qT_psum[:], scalar1=-2.0)
+            squared_norms(q_rows[:, b], q2[:, cols])
+            nc.vector.tensor_scalar_mul(out=neg_q2[:, cols], in0=q2[:, cols], scalar1=-1.0)
+            kT_psum = operand_psum.tile([P, KEYS], BF16, name="transposed")
+            for g in range(PASSES):
+                for u in range(2):
+                    for h in range(2):
+                        col = 512 * g + 256 * u + 128 * h
+                        nc.tensor.transpose(
+                            out=kT_psum[:, col : col + P], in_=k_rows[:, b, u, 2 * g + h, :], identity=ident_bf16[:]
+                        )
+            kT_of[b] = operand_pool.tile([P, KEYS], BF16, name="kT")
+            nc.vector.tensor_copy(out=kT_of[b][:], in_=kT_psum[:])
+            nc.vector.quantize_mx(
+                out=v_codes[:, b, :].bitcast(FP8X4),
+                scales=v_scales[:, b, :],
+                in_=v_grouped[:].rearrange("p g c j -> p (g c j)"),
+            )
+
+        def scores(i):
+            if not 0 <= i < N_TILES:
+                return
+            b, j = divmod(i, TILES_PER_BATCH)
+            for g in range(PASSES):
+                acc = score_psum.tile([P, BANK], F32, name="acc")
+                for u in range(2):
+                    for h in range(2):
+                        col = 256 * u + 128 * h
+                        block = b * TILES_PER_BATCH + 4 * u + 2 * g + h
+                        nc.tensor.matmul(
+                            out=acc[:, col : col + P],
+                            lhsT=k2[:, block : block + 1].to_broadcast([P, P]),
+                            rhs=ident_f32[:],
+                            is_transpose=True,
+                            start=(col == 0),
+                            stop=False,
+                        )
+                nc.tensor.matmul(
+                    out=acc[:],
+                    lhsT=qT_of[b][:, j * P : (j + 1) * P],
+                    rhs=kT_of[b][:, g * BANK : (g + 1) * BANK],
+                    start=False,
+                    stop=True,
+                )
+                acc_of[(i, g)] = acc
+
+        def clamp_and_min(i):
+            if not 0 <= i < N_TILES:
+                return
+            dist_of[i] = dist_pool.tile([P, KEYS], F32, name="dist")
+            for g in range(PASSES):
+                nc.vector.tensor_scalar(
+                    out=dist_of[i][:, g * BANK : (g + 1) * BANK],
+                    in0=acc_of[(i, g)][:],
+                    scalar1=neg_q2[:, i : i + 1],
+                    scalar2=None,
+                    op0=ALU.max,
+                    op1=ALU.min,
+                    accum_out=bank_min[:, i, g : g + 1],
+                )
+
+        def root(i):
+            if not 0 <= i < N_TILES:
+                return
+            nc.scalar.activation(
+                out=dist_of[i][:], in_=dist_of[i][:], func=FUNC.Sqrt, bias=q2[:, i : i + 1], scale=1.0
+            )
+
+        def smallest_distances(first):
+            cols = slice(first, first + PHASE)
+            nc.vector.tensor_reduce(out=row_min[:, cols], in_=bank_min[:, cols, :], axis=AXIS_X, op=ALU.min)
+            nc.vector.tensor_tensor(out=d2_min[:, cols], in0=row_min[:, cols], in1=q2[:, cols], op=ALU.add)
+            nc.scalar.activation(out=dist_min[:, cols], in_=d2_min[:, cols], func=FUNC.Sqrt)
+
+        def weights(i):
+            weight_of[i] = weight_pool.tile([P, KEYS], BF16, name="weight")
+            nc.scalar.activation(
+                out=weight_of[i][:],
+                in_=dist_of[i][:],
+                func=FUNC.Exp,
+                bias=dist_min[:, i : i + 1],
+                scale=-1.0,
+                accum_out=row_sum[:, i : i + 1],
+            )
+
+        def transpose_weights(i):
+            if not 0 <= i < N_TILES:
+                return
+            words = weight_of[i][:].bitcast(F32)
+            wT_of[i] = weight_psum.tile([P, 2 * PASSES, P], F32, name="wT")
+            for n in range(2 * PASSES):
+                nc.tensor.transpose(out=wT_of[i][:, n, :], in_=words[:, n * P : (n + 1) * P], identity=ident_f32[:])
+
+        def regroup(i):
+            if not 0 <= i < N_TILES:
+                return
+            grouped_of[i] = mx_pool.tile([P, KEYS], BF16, name="grouped", align_bytes=64)
+            nc.vector.tensor_copy(
+                out=grouped_of[i][:].bitcast(F32).rearrange("p (g t u) -> p g t u", g=PASSES, u=2),
+                in_=wT_of[i][:].rearrange("p (g u) t -> p g t u", g=PASSES),
+            )
+
+        def quantise(i):
+            if not 0 <= i < N_TILES:
+                return
+            codes_of[i] = mx_pool.tile([P, PASSES * P], U32, name="codes", align_bytes=64)
+            scales_of[i] = mx_pool.tile([P, PASSES * P], U8, name="scales", align_bytes=64)
+            nc.vector.quantize_mx(out=codes_of[i][:].bitcast(FP8X4), scales=scales_of[i][:], in_=grouped_of[i][:])
+
+        def weighted_sum(i):
+            if not 0 <= i < N_TILES:
+                return
+            b = i // TILES_PER_BATCH
+            if i % GROUP == 0:
+                result_of[i // GROUP] = result_psum.tile([P, GROUP, C], F32, name="result")
+            for g in range(PASSES):
+                cols = slice(g * P, (g + 1) * P)
+                nc.tensor.matmul_mx(
+                    out=result_of[i // GROUP][:, i % GROUP, :],
+                    lhsT=codes_of[i][:, cols].bitcast(FP8X4),
+                    lhsT_scale=scales_of[i][:, cols],
+                    rhs=v_codes[:, b, cols].bitcast(FP8X4),
+                    rhs_scale=v_scales[:, b, cols],
+                    start=(g == 0),
+                    stop=(g == PASSES - 1),
+                )
+
+        def invert_sums(last):
+            if not (0 <= last < N_TILES and last % GROUP == GROUP - 1):
+                return
+            cols = slice(last + 1 - GROUP, last + 1)
+            nc.vector.reciprocal(out=inv_sum[:, cols], in_=row_sum[:, cols])
+
+        def divide_and_store(last):
+            if not (0 <= last < N_TILES and last % GROUP == GROUP - 1):
+                return
+            first = last + 1 - GROUP
+            b, j = divmod(first, TILES_PER_BATCH)
+            final = result_pool.tile([P, GROUP, C], F32, name="final")
+            nc.vector.tensor_tensor(
+                out=final[:],
+                in0=result_of[last // GROUP][:],
+                in1=inv_sum[:, first : last + 1].unsqueeze(2).to_broadcast([P, GROUP, C]),
+                op=ALU.mult,
+            )
+            rows = out[b].rearrange("(p j) c -> p j c", j=TILES_PER_BATCH)
+            nc.sync.dma_start(out=rows[:, j : j + GROUP, :], in_=final[:])
+
+        for b in range(BATCHES):
+            load_batch(b)
+        make_identity(nc, ident_bf16[:])
+        make_identity(nc, ident_f32[:])
+        nc.vector.memset(one[:], 1.0)
+        nc.scalar.activation(out=one_root[:], in_=one[:], func=FUNC.Sqrt)
+
+        prepare(0)
+        scores(0)
+        for r in range(N_TILES + LAG + 4):
+            ahead = r + PREPARE_AHEAD
+            if ahead % TILES_PER_BATCH == 0 and ahead < N_TILES:
+                prepare(ahead // TILES_PER_BATCH)
+            weighted_sum(r - LAG - 2)
+            transpose_weights(r - LAG + 1)
+            scores(r + 1)
+            clamp_and_min(r)
+            root(r)
+            regroup(r - LAG)
+            quantise(r - LAG - 1)
+            invert_sums(r - LAG - 2)
+            divide_and_store(r - LAG - 3)
+            if r % PHASE == PHASE - 1 and r < N_TILES:
+                first = r + 1 - PHASE
+                smallest_distances(first)
+                for i in range(first, first + PHASE):
+                    weights(i)

@@ -252,9 +252,9 @@ def tile_qkvattention_pa_kernel(tc, q_scaled, k_scaled, v, out):
             ahead = r + PREPARE_AHEAD
             if ahead % TILES_PER_BATCH == 0 and ahead < N_TILES:
                 prepare(ahead // TILES_PER_BATCH)
-            weighted_sum(r - LAG - 2)
-            transpose_weights(r - LAG + 1)
             scores(r + 1)
+            transpose_weights(r - LAG + 1)
+            weighted_sum(r - LAG - 2)
             clamp_and_min(r)
             root(r)
             regroup(r - LAG)

@@ -21,9 +21,9 @@ N_TILES = BATCHES * TILES_PER_BATCH
 GROUP = 4
 
 PHASE = 16
-LAG = PHASE + 2
-DIST_BUFS = PHASE + 3
-WEIGHT_BUFS = 11
+LAG = PHASE + 4
+DIST_BUFS = PHASE + 5
+WEIGHT_BUFS = 13
 PREPARE_AHEAD = 3
 
 FLOPS = 2 * 2 * BATCHES * KEYS * KEYS * C
@@ -33,7 +33,8 @@ def tile_qkvattention_pa_kernel(tc, q_scaled, k_scaled, v, out):
     nc = tc.nc
     with ExitStack() as ctx:
         keep = ctx.enter_context(tc.tile_pool(name="keep", bufs=1))
-        square_pool = ctx.enter_context(tc.tile_pool(name="squares", bufs=2))
+        scratch_pool = ctx.enter_context(tc.tile_pool(name="scratch", bufs=1))
+        ahead_pool = ctx.enter_context(tc.tile_pool(name="ahead", bufs=3))
         operand_pool = ctx.enter_context(tc.tile_pool(name="operands", bufs=2))
         dist_pool = ctx.enter_context(tc.tile_pool(name="distances", bufs=DIST_BUFS))
         weight_pool = ctx.enter_context(tc.tile_pool(name="weights", bufs=WEIGHT_BUFS))
@@ -77,22 +78,39 @@ def tile_qkvattention_pa_kernel(tc, q_scaled, k_scaled, v, out):
             )
             nc.sync.dma_start(out=v_rows[:, b], in_=v[b].rearrange("(g p j) c -> p g j c", g=PASSES, j=4))
 
-        def squared_norms(rows, sums):
-            squares = square_pool.tile([P, TILES_PER_BATCH, C], F32, name="squares")
+        def squares_folded(rows, name):
+            squares = scratch_pool.tile([P, TILES_PER_BATCH, C], F32, name="squares")
             nc.gpsimd.tensor_tensor(out=squares[:], in0=rows, in1=rows, op=ALU.mult)
-            nc.vector.tensor_reduce(out=sums, in_=squares[:], axis=AXIS_X, op=ALU.add)
+            halves = scratch_pool.tile([P, TILES_PER_BATCH, C // 2], F32, name="halves")
+            nc.gpsimd.tensor_tensor(
+                out=halves[:], in0=squares[:, :, : C // 2], in1=squares[:, :, C // 2 :], op=ALU.add
+            )
+            quarters = ahead_pool.tile([P, TILES_PER_BATCH, C // 4], F32, name=name)
+            nc.gpsimd.tensor_tensor(
+                out=quarters[:], in0=halves[:, :, : C // 4], in1=halves[:, :, C // 4 :], op=ALU.add
+            )
+            return quarters
 
         def prepare(b):
             cols = slice(b * TILES_PER_BATCH, (b + 1) * TILES_PER_BATCH)
-            v_grouped = operand_pool.tile([P, PASSES, C, 4], BF16, name="v_grouped", align_bytes=64)
-            nc.vector.tensor_copy(out=v_grouped[:], in_=v_rows[:, b].rearrange("p g j c -> p g c j"))
-            squared_norms(k_rows[:, b].rearrange("p u a c -> p (u a) c"), k2[:, cols])
+            k_quarters = squares_folded(k_rows[:, b].rearrange("p u a c -> p (u a) c"), "k_quarters")
+            q_quarters = squares_folded(q_rows[:, b], "q_quarters")
+            v_grouped = ahead_pool.tile([P, PASSES, C, 4], BF16, name="v_grouped", align_bytes=64)
+            nc.gpsimd.tensor_scalar(
+                out=v_grouped[:],
+                in0=v_rows[:, b].rearrange("p g j c -> p g c j"),
+                scalar1=1.0,
+                scalar2=0.0,
+                op0=ALU.mult,
+                op1=ALU.add,
+            )
+            nc.vector.tensor_reduce(out=k2[:, cols], in_=k_quarters[:], axis=AXIS_X, op=ALU.add)
             qT_psum = operand_psum.tile([P, KEYS], BF16, name="transposed")
             for j in range(TILES_PER_BATCH):
                 nc.tensor.transpose(out=qT_psum[:, j * P : (j + 1) * P], in_=q_rows[:, b, j, :], identity=ident_bf16[:])
             qT_of[b] = operand_pool.tile([P, KEYS], BF16, name="qT")
             nc.vector.tensor_scalar_mul(out=qT_of[b][:], in0=qT_psum[:], scalar1=-2.0)
-            squared_norms(q_rows[:, b], q2[:, cols])
+            nc.vector.tensor_reduce(out=q2[:, cols], in_=q_quarters[:], axis=AXIS_X, op=ALU.add)
             nc.vector.tensor_scalar_mul(out=neg_q2[:, cols], in0=q2[:, cols], scalar1=-1.0)
             kT_psum = operand_psum.tile([P, KEYS], BF16, name="transposed")
             for g in range(PASSES):

@@ -24,7 +24,7 @@ PHASE = 16
 LAG = PHASE + 4
 DIST_BUFS = PHASE + 5
 WEIGHT_BUFS = 13
-PREPARE_AHEAD = 3
+PREPARE_AHEAD = 4
 
 FLOPS = 2 * 2 * BATCHES * KEYS * KEYS * C
 
@@ -33,7 +33,7 @@ def tile_qkvattention_pa_kernel(tc, q_scaled, k_scaled, v, out):
     nc = tc.nc
     with ExitStack() as ctx:
         keep = ctx.enter_context(tc.tile_pool(name="keep", bufs=1))
-        scratch_pool = ctx.enter_context(tc.tile_pool(name="scratch", bufs=1))
+        scratch_pool = ctx.enter_context(tc.tile_pool(name="scratch", bufs=2))
         ahead_pool = ctx.enter_context(tc.tile_pool(name="ahead", bufs=3))
         operand_pool = ctx.enter_context(tc.tile_pool(name="operands", bufs=2))
         dist_pool = ctx.enter_context(tc.tile_pool(name="distances", bufs=DIST_BUFS))
@@ -67,6 +67,7 @@ def tile_qkvattention_pa_kernel(tc, q_scaled, k_scaled, v, out):
 
         qT_of, kT_of, acc_of, dist_of, weight_of = {}, {}, {}, {}, {}
         wT_of, grouped_of, codes_of, scales_of, result_of = {}, {}, {}, {}, {}
+        partial_of, v_grouped_of, transposed_of = {}, {}, {}
 
         def load_batch(b):
             k_view = k_scaled[b].rearrange("(a m u e) c -> u e m a c", a=4, m=64, u=2, e=2)
@@ -78,55 +79,63 @@ def tile_qkvattention_pa_kernel(tc, q_scaled, k_scaled, v, out):
             )
             nc.sync.dma_start(out=v_rows[:, b], in_=v[b].rearrange("(g p j) c -> p g j c", g=PASSES, j=4))
 
-        def squares_folded(rows, name):
-            squares = scratch_pool.tile([P, TILES_PER_BATCH, C], F32, name="squares")
-            nc.gpsimd.tensor_tensor(out=squares[:], in0=rows, in1=rows, op=ALU.mult)
-            halves = scratch_pool.tile([P, TILES_PER_BATCH, C // 2], F32, name="halves")
-            nc.gpsimd.tensor_tensor(
-                out=halves[:], in0=squares[:, :, : C // 2], in1=squares[:, :, C // 2 :], op=ALU.add
-            )
-            quarters = ahead_pool.tile([P, TILES_PER_BATCH, C // 4], F32, name=name)
-            nc.gpsimd.tensor_tensor(
-                out=quarters[:], in0=halves[:, :, : C // 4], in1=halves[:, :, C // 4 :], op=ALU.add
-            )
-            return quarters
+        def squares(rows):
+            wide = scratch_pool.tile([P, TILES_PER_BATCH, C], F32, name="squares")
+            nc.gpsimd.tensor_tensor(out=wide[:], in0=rows, in1=rows, op=ALU.mult)
+            return wide
 
-        def prepare(b):
+        def fold(wide, pool, name):
+            width = wide.shape[2] // 2
+            narrow = pool.tile([P, TILES_PER_BATCH, width], F32, name=name)
+            nc.gpsimd.tensor_tensor(out=narrow[:], in0=wide[:, :, :width], in1=wide[:, :, width:], op=ALU.add)
+            return narrow
+
+        def prepare(b, step):
             cols = slice(b * TILES_PER_BATCH, (b + 1) * TILES_PER_BATCH)
-            k_quarters = squares_folded(k_rows[:, b].rearrange("p u a c -> p (u a) c"), "k_quarters")
-            q_quarters = squares_folded(q_rows[:, b], "q_quarters")
-            v_grouped = ahead_pool.tile([P, PASSES, C, 4], BF16, name="v_grouped", align_bytes=64)
-            nc.gpsimd.tensor_scalar(
-                out=v_grouped[:],
-                in0=v_rows[:, b].rearrange("p g j c -> p g c j"),
-                scalar1=1.0,
-                scalar2=0.0,
-                op0=ALU.mult,
-                op1=ALU.add,
-            )
-            nc.vector.tensor_reduce(out=k2[:, cols], in_=k_quarters[:], axis=AXIS_X, op=ALU.add)
-            qT_psum = operand_psum.tile([P, KEYS], BF16, name="transposed")
-            for j in range(TILES_PER_BATCH):
-                nc.tensor.transpose(out=qT_psum[:, j * P : (j + 1) * P], in_=q_rows[:, b, j, :], identity=ident_bf16[:])
-            qT_of[b] = operand_pool.tile([P, KEYS], BF16, name="qT")
-            nc.vector.tensor_scalar_mul(out=qT_of[b][:], in0=qT_psum[:], scalar1=-2.0)
-            nc.vector.tensor_reduce(out=q2[:, cols], in_=q_quarters[:], axis=AXIS_X, op=ALU.add)
-            nc.vector.tensor_scalar_mul(out=neg_q2[:, cols], in0=q2[:, cols], scalar1=-1.0)
-            kT_psum = operand_psum.tile([P, KEYS], BF16, name="transposed")
-            for g in range(PASSES):
-                for u in range(2):
-                    for h in range(2):
-                        col = 512 * g + 256 * u + 128 * h
-                        nc.tensor.transpose(
-                            out=kT_psum[:, col : col + P], in_=k_rows[:, b, u, 2 * g + h, :], identity=ident_bf16[:]
-                        )
-            kT_of[b] = operand_pool.tile([P, KEYS], BF16, name="kT")
-            nc.vector.tensor_copy(out=kT_of[b][:], in_=kT_psum[:])
-            nc.vector.quantize_mx(
-                out=v_codes[:, b, :].bitcast(FP8X4),
-                scales=v_scales[:, b, :],
-                in_=v_grouped[:].rearrange("p g c j -> p (g c j)"),
-            )
+            if step == 0:
+                for name, rows in (("k", k_rows[:, b].rearrange("p u a c -> p (u a) c")), ("q", q_rows[:, b])):
+                    sums = squares(rows)
+                    if b > 0:
+                        sums = fold(fold(sums, scratch_pool, "halves"), ahead_pool, name + "_quarters")
+                    partial_of[(name, b)] = sums
+                v_grouped_of[b] = ahead_pool.tile([P, PASSES, C, 4], BF16, name="v_grouped", align_bytes=64)
+                nc.gpsimd.tensor_scalar(
+                    out=v_grouped_of[b][:],
+                    in0=v_rows[:, b].rearrange("p g j c -> p g c j"),
+                    scalar1=1.0,
+                    scalar2=0.0,
+                    op0=ALU.mult,
+                    op1=ALU.add,
+                )
+                transposed_of[b] = operand_psum.tile([P, KEYS], BF16, name="transposed")
+                for j in range(TILES_PER_BATCH):
+                    nc.tensor.transpose(
+                        out=transposed_of[b][:, j * P : (j + 1) * P], in_=q_rows[:, b, j, :], identity=ident_bf16[:]
+                    )
+            if step == 1:
+                qT_of[b] = operand_pool.tile([P, KEYS], BF16, name="qT")
+                nc.vector.tensor_scalar_mul(out=qT_of[b][:], in0=transposed_of[b][:], scalar1=-2.0)
+                nc.vector.tensor_reduce(out=k2[:, cols], in_=partial_of[("k", b)][:], axis=AXIS_X, op=ALU.add)
+                transposed_of[b] = operand_psum.tile([P, KEYS], BF16, name="transposed")
+                for g in range(PASSES):
+                    for u in range(2):
+                        for h in range(2):
+                            col = 512 * g + 256 * u + 128 * h
+                            nc.tensor.transpose(
+                                out=transposed_of[b][:, col : col + P],
+                                in_=k_rows[:, b, u, 2 * g + h, :],
+                                identity=ident_bf16[:],
+                            )
+            if step == 2:
+                kT_of[b] = operand_pool.tile([P, KEYS], BF16, name="kT")
+                nc.vector.tensor_copy(out=kT_of[b][:], in_=transposed_of[b][:])
+                nc.vector.tensor_reduce(out=q2[:, cols], in_=partial_of[("q", b)][:], axis=AXIS_X, op=ALU.add)
+                nc.vector.tensor_scalar_mul(out=neg_q2[:, cols], in0=q2[:, cols], scalar1=-1.0)
+                nc.vector.quantize_mx(
+                    out=v_codes[:, b, :].bitcast(FP8X4),
+                    scales=v_scales[:, b, :],
+                    in_=v_grouped_of[b][:].rearrange("p g c j -> p (g c j)"),
+                )
 
         def scores(i):
             if not 0 <= i < N_TILES:
@@ -264,17 +273,18 @@ def tile_qkvattention_pa_kernel(tc, q_scaled, k_scaled, v, out):
         nc.vector.memset(one[:], 1.0)
         nc.scalar.activation(out=one_root[:], in_=one[:], func=FUNC.Sqrt)
 
-        prepare(0)
+        for step in range(3):
+            prepare(0, step)
         scores(0)
         for r in range(N_TILES + LAG + 4):
-            ahead = r + PREPARE_AHEAD
-            if ahead % TILES_PER_BATCH == 0 and ahead < N_TILES:
-                prepare(ahead // TILES_PER_BATCH)
             scores(r + 1)
             transpose_weights(r - LAG + 1)
             weighted_sum(r - LAG - 2)
             clamp_and_min(r)
             root(r)
+            b, step = divmod(r + PREPARE_AHEAD, TILES_PER_BATCH)
+            if 0 < b < BATCHES:
+                prepare(b, step)
             regroup(r - LAG)
             quantise(r - LAG - 1)
             invert_sums(r - LAG - 2)

@@ -24,6 +24,7 @@ PHASE = 16
 LAG = PHASE + 4
 DIST_BUFS = PHASE + 5
 WEIGHT_BUFS = 13
+REGROUP_V_AT = 5
 PREPARE_AHEAD = 4
 
 FLOPS = 2 * 2 * BATCHES * KEYS * KEYS * C
@@ -34,15 +35,15 @@ def tile_qkvattention_pa_kernel(tc, q_scaled, k_scaled, v, out):
     with ExitStack() as ctx:
         keep = ctx.enter_context(tc.tile_pool(name="keep", bufs=1))
         scratch_pool = ctx.enter_context(tc.tile_pool(name="scratch", bufs=2))
-        ahead_pool = ctx.enter_context(tc.tile_pool(name="ahead", bufs=3))
+        ahead_pool = ctx.enter_context(tc.tile_pool(name="ahead", bufs=2))
         operand_pool = ctx.enter_context(tc.tile_pool(name="operands", bufs=2))
         dist_pool = ctx.enter_context(tc.tile_pool(name="distances", bufs=DIST_BUFS))
         weight_pool = ctx.enter_context(tc.tile_pool(name="weights", bufs=WEIGHT_BUFS))
         mx_pool = ctx.enter_context(tc.tile_pool(name="mx", bufs=3))
         result_pool = ctx.enter_context(tc.tile_pool(name="results", bufs=3))
-        score_psum = ctx.enter_context(tc.psum_pool(name="score_psum", bufs=4))
+        score_psum = ctx.enter_context(tc.psum_pool(name="score_psum", bufs=3))
         weight_psum = ctx.enter_context(tc.psum_pool(name="weight_psum", bufs=2))
-        result_psum = ctx.enter_context(tc.psum_pool(name="result_psum", bufs=1))
+        result_psum = ctx.enter_context(tc.psum_pool(name="result_psum", bufs=2))
         operand_psum = ctx.enter_context(tc.psum_pool(name="operand_psum", bufs=1))
         ctx.enter_context(tc.manual_schedule())
 
@@ -67,7 +68,7 @@ def tile_qkvattention_pa_kernel(tc, q_scaled, k_scaled, v, out):
 
         qT_of, kT_of, acc_of, dist_of, weight_of = {}, {}, {}, {}, {}
         wT_of, grouped_of, codes_of, scales_of, result_of = {}, {}, {}, {}, {}
-        partial_of, v_grouped_of, transposed_of = {}, {}, {}
+        v_grouped_of, transposed_of = {}, {}
 
         def load_batch(b):
             k_view = k_scaled[b].rearrange("(a m u e) c -> u e m a c", a=4, m=64, u=2, e=2)
@@ -79,34 +80,34 @@ def tile_qkvattention_pa_kernel(tc, q_scaled, k_scaled, v, out):
             )
             nc.sync.dma_start(out=v_rows[:, b], in_=v[b].rearrange("(g p j) c -> p g j c", g=PASSES, j=4))
 
-        def squares(rows):
+        def squared_norms(b, rows, sums):
             wide = scratch_pool.tile([P, TILES_PER_BATCH, C], F32, name="squares")
             nc.gpsimd.tensor_tensor(out=wide[:], in0=rows, in1=rows, op=ALU.mult)
-            return wide
+            if b == 0:
+                nc.vector.tensor_reduce(out=sums, in_=wide[:], axis=AXIS_X, op=ALU.add)
+                return
+            width = C // 2
+            while width > 1:
+                narrow = scratch_pool.tile([P, TILES_PER_BATCH, width], F32, name="fold%d" % width)
+                nc.gpsimd.tensor_tensor(out=narrow[:], in0=wide[:, :, :width], in1=wide[:, :, width:], op=ALU.add)
+                wide = narrow
+                width //= 2
+            nc.gpsimd.tensor_tensor(out=sums.unsqueeze(2), in0=wide[:, :, 0:1], in1=wide[:, :, 1:2], op=ALU.add)
 
-        def fold(wide, pool, name):
-            width = wide.shape[2] // 2
-            narrow = pool.tile([P, TILES_PER_BATCH, width], F32, name=name)
-            nc.gpsimd.tensor_tensor(out=narrow[:], in0=wide[:, :, :width], in1=wide[:, :, width:], op=ALU.add)
-            return narrow
+        def key_norms(b):
+            cols = slice(b * TILES_PER_BATCH, (b + 1) * TILES_PER_BATCH)
+            squared_norms(b, k_rows[:, b].rearrange("p u a c -> p (u a) c"), k2[:, cols])
+
+        def query_norms(b):
+            cols = slice(b * TILES_PER_BATCH, (b + 1) * TILES_PER_BATCH)
+            squared_norms(b, q_rows[:, b], q2[:, cols])
+            engine = nc.vector if b == 0 else nc.gpsimd
+            engine.tensor_scalar(
+                out=neg_q2[:, cols], in0=q2[:, cols], scalar1=-1.0, scalar2=0.0, op0=ALU.mult, op1=ALU.add
+            )
 
         def prepare(b, step):
-            cols = slice(b * TILES_PER_BATCH, (b + 1) * TILES_PER_BATCH)
             if step == 0:
-                for name, rows in (("k", k_rows[:, b].rearrange("p u a c -> p (u a) c")), ("q", q_rows[:, b])):
-                    sums = squares(rows)
-                    if b > 0:
-                        sums = fold(fold(sums, scratch_pool, "halves"), ahead_pool, name + "_quarters")
-                    partial_of[(name, b)] = sums
-                v_grouped_of[b] = ahead_pool.tile([P, PASSES, C, 4], BF16, name="v_grouped", align_bytes=64)
-                nc.gpsimd.tensor_scalar(
-                    out=v_grouped_of[b][:],
-                    in0=v_rows[:, b].rearrange("p g j c -> p g c j"),
-                    scalar1=1.0,
-                    scalar2=0.0,
-                    op0=ALU.mult,
-                    op1=ALU.add,
-                )
                 transposed_of[b] = operand_psum.tile([P, KEYS], BF16, name="transposed")
                 for j in range(TILES_PER_BATCH):
                     nc.tensor.transpose(
@@ -115,7 +116,6 @@ def tile_qkvattention_pa_kernel(tc, q_scaled, k_scaled, v, out):
             if step == 1:
                 qT_of[b] = operand_pool.tile([P, KEYS], BF16, name="qT")
                 nc.vector.tensor_scalar_mul(out=qT_of[b][:], in0=transposed_of[b][:], scalar1=-2.0)
-                nc.vector.tensor_reduce(out=k2[:, cols], in_=partial_of[("k", b)][:], axis=AXIS_X, op=ALU.add)
                 transposed_of[b] = operand_psum.tile([P, KEYS], BF16, name="transposed")
                 for g in range(PASSES):
                     for u in range(2):
@@ -129,13 +129,24 @@ def tile_qkvattention_pa_kernel(tc, q_scaled, k_scaled, v, out):
             if step == 2:
                 kT_of[b] = operand_pool.tile([P, KEYS], BF16, name="kT")
                 nc.vector.tensor_copy(out=kT_of[b][:], in_=transposed_of[b][:])
-                nc.vector.tensor_reduce(out=q2[:, cols], in_=partial_of[("q", b)][:], axis=AXIS_X, op=ALU.add)
-                nc.vector.tensor_scalar_mul(out=neg_q2[:, cols], in0=q2[:, cols], scalar1=-1.0)
-                nc.vector.quantize_mx(
-                    out=v_codes[:, b, :].bitcast(FP8X4),
-                    scales=v_scales[:, b, :],
-                    in_=v_grouped_of[b][:].rearrange("p g c j -> p (g c j)"),
-                )
+
+        def regroup_v(b):
+            v_grouped_of[b] = ahead_pool.tile([P, PASSES, C, 4], BF16, name="v_grouped", align_bytes=64)
+            nc.gpsimd.tensor_scalar(
+                out=v_grouped_of[b][:],
+                in0=v_rows[:, b].rearrange("p g j c -> p g c j"),
+                scalar1=1.0,
+                scalar2=0.0,
+                op0=ALU.mult,
+                op1=ALU.add,
+            )
+
+        def quantise_v(b):
+            nc.vector.quantize_mx(
+                out=v_codes[:, b, :].bitcast(FP8X4),
+                scales=v_scales[:, b, :],
+                in_=v_grouped_of[b][:].rearrange("p g c j -> p (g c j)"),
+            )
 
         def scores(i):
             if not 0 <= i < N_TILES:
@@ -273,8 +284,11 @@ def tile_qkvattention_pa_kernel(tc, q_scaled, k_scaled, v, out):
         nc.vector.memset(one[:], 1.0)
         nc.scalar.activation(out=one_root[:], in_=one[:], func=FUNC.Sqrt)
 
-        for step in range(3):
-            prepare(0, step)
+        prepare(0, 0)
+        prepare(0, 1)
+        key_norms(0)
+        prepare(0, 2)
+        query_norms(0)
         scores(0)
         for r in range(N_TILES + LAG + 4):
             scores(r + 1)
@@ -284,7 +298,15 @@ def tile_qkvattention_pa_kernel(tc, q_scaled, k_scaled, v, out):
             root(r)
             b, step = divmod(r + PREPARE_AHEAD, TILES_PER_BATCH)
             if 0 < b < BATCHES:
+                if step == 0:
+                    key_norms(b)
+                    query_norms(b)
                 prepare(b, step)
+            b, step = divmod(r, TILES_PER_BATCH)
+            if b < BATCHES and step == REGROUP_V_AT:
+                regroup_v(b)
+            if b < BATCHES and step == REGROUP_V_AT + 2:
+                quantise_v(b)
             regroup(r - LAG)
             quantise(r - LAG - 1)
             invert_sums(r - LAG - 2)

@@ -24,7 +24,7 @@ PHASE = 16
 LAG = PHASE + 4
 DIST_BUFS = PHASE + 5
 WEIGHT_BUFS = 13
-REGROUP_V_AT = 5
+NORM_ROUNDS = 3
 PREPARE_AHEAD = 4
 
 FLOPS = 2 * 2 * BATCHES * KEYS * KEYS * C
@@ -35,15 +35,15 @@ def tile_qkvattention_pa_kernel(tc, q_scaled, k_scaled, v, out):
     with ExitStack() as ctx:
         keep = ctx.enter_context(tc.tile_pool(name="keep", bufs=1))
         scratch_pool = ctx.enter_context(tc.tile_pool(name="scratch", bufs=2))
-        ahead_pool = ctx.enter_context(tc.tile_pool(name="ahead", bufs=2))
+        quarter_pool = ctx.enter_context(tc.tile_pool(name="quarters", bufs=NORM_ROUNDS + 1))
         operand_pool = ctx.enter_context(tc.tile_pool(name="operands", bufs=2))
         dist_pool = ctx.enter_context(tc.tile_pool(name="distances", bufs=DIST_BUFS))
         weight_pool = ctx.enter_context(tc.tile_pool(name="weights", bufs=WEIGHT_BUFS))
         mx_pool = ctx.enter_context(tc.tile_pool(name="mx", bufs=3))
         result_pool = ctx.enter_context(tc.tile_pool(name="results", bufs=3))
-        score_psum = ctx.enter_context(tc.psum_pool(name="score_psum", bufs=3))
+        score_psum = ctx.enter_context(tc.psum_pool(name="score_psum", bufs=4))
         weight_psum = ctx.enter_context(tc.psum_pool(name="weight_psum", bufs=2))
-        result_psum = ctx.enter_context(tc.psum_pool(name="result_psum", bufs=2))
+        result_psum = ctx.enter_context(tc.psum_pool(name="result_psum", bufs=1))
         operand_psum = ctx.enter_context(tc.psum_pool(name="operand_psum", bufs=1))
         ctx.enter_context(tc.manual_schedule())
 
@@ -52,6 +52,7 @@ def tile_qkvattention_pa_kernel(tc, q_scaled, k_scaled, v, out):
         q_rows = keep.tile([P, BATCHES, TILES_PER_BATCH, C], BF16)
         k_rows = keep.tile([P, BATCHES, 2, 4, C], BF16)
         v_rows = keep.tile([P, BATCHES, PASSES, 4, C], BF16)
+        v_grouped = keep.tile([P, BATCHES, PASSES, C, 4], BF16, align_bytes=64)
         v_codes = keep.tile([P, BATCHES, PASSES * C], U32, align_bytes=64)
         v_scales = keep.tile([P, BATCHES, PASSES * C], U8, align_bytes=64)
         q2 = keep.tile([P, N_TILES], F32)
@@ -68,7 +69,7 @@ def tile_qkvattention_pa_kernel(tc, q_scaled, k_scaled, v, out):
 
         qT_of, kT_of, acc_of, dist_of, weight_of = {}, {}, {}, {}, {}
         wT_of, grouped_of, codes_of, scales_of, result_of = {}, {}, {}, {}, {}
-        v_grouped_of, transposed_of = {}, {}
+        partial_of, transposed_of = {}, {}
 
         def load_batch(b):
             k_view = k_scaled[b].rearrange("(a m u e) c -> u e m a c", a=4, m=64, u=2, e=2)
@@ -80,31 +81,39 @@ def tile_qkvattention_pa_kernel(tc, q_scaled, k_scaled, v, out):
             )
             nc.sync.dma_start(out=v_rows[:, b], in_=v[b].rearrange("(g p j) c -> p g j c", g=PASSES, j=4))
 
-        def squared_norms(b, rows, sums):
-            wide = scratch_pool.tile([P, TILES_PER_BATCH, C], F32, name="squares")
-            nc.gpsimd.tensor_tensor(out=wide[:], in0=rows, in1=rows, op=ALU.mult)
-            if b == 0:
-                nc.vector.tensor_reduce(out=sums, in_=wide[:], axis=AXIS_X, op=ALU.add)
+        def norm_operands(n):
+            b = n // 2
+            cols = slice(b * TILES_PER_BATCH, (b + 1) * TILES_PER_BATCH)
+            if n % 2 == 0:
+                return k_rows[:, b].rearrange("p u a c -> p (u a) c"), k2[:, cols]
+            return q_rows[:, b], q2[:, cols]
+
+        def fold(wide, pool, name):
+            width = wide.shape[2] // 2
+            narrow = pool.tile([P, TILES_PER_BATCH, width], F32, name=name)
+            nc.gpsimd.tensor_tensor(out=narrow[:], in0=wide[:, :, :width], in1=wide[:, :, width:], op=ALU.add)
+            return narrow
+
+        def start_norms(n):
+            if not 0 <= n < 2 * BATCHES:
                 return
-            width = C // 2
-            while width > 1:
-                narrow = scratch_pool.tile([P, TILES_PER_BATCH, width], F32, name="fold%d" % width)
-                nc.gpsimd.tensor_tensor(out=narrow[:], in0=wide[:, :, :width], in1=wide[:, :, width:], op=ALU.add)
-                wide = narrow
-                width //= 2
-            nc.gpsimd.tensor_tensor(out=sums.unsqueeze(2), in0=wide[:, :, 0:1], in1=wide[:, :, 1:2], op=ALU.add)
+            rows = norm_operands(n)[0]
+            squares = scratch_pool.tile([P, TILES_PER_BATCH, C], F32, name="squares")
+            nc.scalar.activation(out=squares[:], in_=rows, func=FUNC.Square)
+            if n < 2:
+                partial_of[n] = squares
+            else:
+                partial_of[n] = fold(fold(squares, scratch_pool, "halves"), quarter_pool, "quarters")
 
-        def key_norms(b):
-            cols = slice(b * TILES_PER_BATCH, (b + 1) * TILES_PER_BATCH)
-            squared_norms(b, k_rows[:, b].rearrange("p u a c -> p (u a) c"), k2[:, cols])
-
-        def query_norms(b):
-            cols = slice(b * TILES_PER_BATCH, (b + 1) * TILES_PER_BATCH)
-            squared_norms(b, q_rows[:, b], q2[:, cols])
-            engine = nc.vector if b == 0 else nc.gpsimd
-            engine.tensor_scalar(
-                out=neg_q2[:, cols], in0=q2[:, cols], scalar1=-1.0, scalar2=0.0, op0=ALU.mult, op1=ALU.add
-            )
+        def finish_norms(n):
+            if not 0 <= n < 2 * BATCHES:
+                return
+            sums = norm_operands(n)[1]
+            nc.vector.tensor_reduce(out=sums, in_=partial_of[n][:], axis=AXIS_X, op=ALU.add)
+            if n % 2 == 1:
+                b = n // 2
+                cols = slice(b * TILES_PER_BATCH, (b + 1) * TILES_PER_BATCH)
+                nc.vector.tensor_scalar_mul(out=neg_q2[:, cols], in0=sums, scalar1=-1.0)
 
         def prepare(b, step):
             if step == 0:
@@ -131,9 +140,10 @@ def tile_qkvattention_pa_kernel(tc, q_scaled, k_scaled, v, out):
                 nc.vector.tensor_copy(out=kT_of[b][:], in_=transposed_of[b][:])
 
         def regroup_v(b):
-            v_grouped_of[b] = ahead_pool.tile([P, PASSES, C, 4], BF16, name="v_grouped", align_bytes=64)
+            if not 0 <= b < BATCHES:
+                return
             nc.gpsimd.tensor_scalar(
-                out=v_grouped_of[b][:],
+                out=v_grouped[:, b],
                 in0=v_rows[:, b].rearrange("p g j c -> p g c j"),
                 scalar1=1.0,
                 scalar2=0.0,
@@ -145,7 +155,7 @@ def tile_qkvattention_pa_kernel(tc, q_scaled, k_scaled, v, out):
             nc.vector.quantize_mx(
                 out=v_codes[:, b, :].bitcast(FP8X4),
                 scales=v_scales[:, b, :],
-                in_=v_grouped_of[b][:].rearrange("p g c j -> p (g c j)"),
+                in_=v_grouped[:, b].rearrange("p g c j -> p (g c j)"),
             )
 
         def scores(i):
@@ -284,11 +294,13 @@ def tile_qkvattention_pa_kernel(tc, q_scaled, k_scaled, v, out):
         nc.vector.memset(one[:], 1.0)
         nc.scalar.activation(out=one_root[:], in_=one[:], func=FUNC.Sqrt)
 
+        start_norms(0)
+        start_norms(1)
         prepare(0, 0)
         prepare(0, 1)
-        key_norms(0)
+        finish_norms(0)
         prepare(0, 2)
-        query_norms(0)
+        finish_norms(1)
         scores(0)
         for r in range(N_TILES + LAG + 4):
             scores(r + 1)
@@ -296,16 +308,15 @@ def tile_qkvattention_pa_kernel(tc, q_scaled, k_scaled, v, out):
             weighted_sum(r - LAG - 2)
             clamp_and_min(r)
             root(r)
+            start_norms(r + 2)
+            if r >= NORM_ROUNDS:
+                finish_norms(r + 2 - NORM_ROUNDS)
+            regroup_v(r + 2 - 2 * BATCHES)
             b, step = divmod(r + PREPARE_AHEAD, TILES_PER_BATCH)
             if 0 < b < BATCHES:
-                if step == 0:
-                    key_norms(b)
-                    query_norms(b)
                 prepare(b, step)
-            b, step = divmod(r, TILES_PER_BATCH)
-            if b < BATCHES and step == REGROUP_V_AT:
-                regroup_v(b)
-            if b < BATCHES and step == REGROUP_V_AT + 2:
+            b, step = divmod(r - (LAG - 2), TILES_PER_BATCH)
+            if 0 <= b < BATCHES and step == 0:
                 quantise_v(b)
             regroup(r - LAG)
             quantise(r - LAG - 1)

@@ -40,6 +40,7 @@ def tile_qkvattention_pa_kernel(tc, q_scaled, k_scaled, v, out):
         dist_pool = ctx.enter_context(tc.tile_pool(name="distances", bufs=DIST_BUFS))
         weight_pool = ctx.enter_context(tc.tile_pool(name="weights", bufs=WEIGHT_BUFS))
         mx_pool = ctx.enter_context(tc.tile_pool(name="mx", bufs=3))
+        code_pool = ctx.enter_context(tc.tile_pool(name="code", bufs=GROUP + 2))
         result_pool = ctx.enter_context(tc.tile_pool(name="results", bufs=3))
         score_psum = ctx.enter_context(tc.psum_pool(name="score_psum", bufs=4))
         weight_psum = ctx.enter_context(tc.psum_pool(name="weight_psum", bufs=2))
@@ -244,27 +245,27 @@ def tile_qkvattention_pa_kernel(tc, q_scaled, k_scaled, v, out):
         def quantise(i):
             if not 0 <= i < N_TILES:
                 return
-            codes_of[i] = mx_pool.tile([P, PASSES * P], U32, name="codes", align_bytes=64)
-            scales_of[i] = mx_pool.tile([P, PASSES * P], U8, name="scales", align_bytes=64)
+            codes_of[i] = code_pool.tile([P, PASSES * P], U32, name="codes", align_bytes=64)
+            scales_of[i] = code_pool.tile([P, PASSES * P], U8, name="scales", align_bytes=64)
             nc.vector.quantize_mx(out=codes_of[i][:].bitcast(FP8X4), scales=scales_of[i][:], in_=grouped_of[i][:])
 
-        def weighted_sum(i):
-            if not 0 <= i < N_TILES:
+        def weighted_sums(last):
+            if not (0 <= last < N_TILES and last % GROUP == GROUP - 1):
                 return
-            b = i // TILES_PER_BATCH
-            if i % GROUP == 0:
-                result_of[i // GROUP] = result_psum.tile([P, GROUP, C], F32, name="result")
-            for g in range(PASSES):
-                cols = slice(g * P, (g + 1) * P)
-                nc.tensor.matmul_mx(
-                    out=result_of[i // GROUP][:, i % GROUP, :],
-                    lhsT=codes_of[i][:, cols].bitcast(FP8X4),
-                    lhsT_scale=scales_of[i][:, cols],
-                    rhs=v_codes[:, b, cols].bitcast(FP8X4),
-                    rhs_scale=v_scales[:, b, cols],
-                    start=(g == 0),
-                    stop=(g == PASSES - 1),
-                )
+            b = last // TILES_PER_BATCH
+            result_of[last // GROUP] = result_psum.tile([P, GROUP, C], F32, name="result")
+            for i in range(last + 1 - GROUP, last + 1):
+                for g in range(PASSES):
+                    cols = slice(g * P, (g + 1) * P)
+                    nc.tensor.matmul_mx(
+                        out=result_of[last // GROUP][:, i % GROUP, :],
+                        lhsT=codes_of[i][:, cols].bitcast(FP8X4),
+                        lhsT_scale=scales_of[i][:, cols],
+                        rhs=v_codes[:, b, cols].bitcast(FP8X4),
+                        rhs_scale=v_scales[:, b, cols],
+                        start=(g == 0),
+                        stop=(g == PASSES - 1),
+                    )
 
         def invert_sums(last):
             if not (0 <= last < N_TILES and last % GROUP == GROUP - 1):
@@ -305,7 +306,7 @@ def tile_qkvattention_pa_kernel(tc, q_scaled, k_scaled, v, out):
         for r in range(N_TILES + LAG + 4):
             scores(r + 1)
             transpose_weights(r - LAG + 1)
-            weighted_sum(r - LAG - 2)
+            weighted_sums(r - LAG - 2)
             clamp_and_min(r)
             root(r)
             start_norms(r + 2)

@@ -24,7 +24,8 @@ PHASE = 16
 LAG = PHASE + 4
 DIST_BUFS = PHASE + 5
 WEIGHT_BUFS = 13
-NORM_ROUNDS = 3
+SCALAR_SQUARES = 4
+NORMS_AHEAD = 6
 PREPARE_AHEAD = 4
 
 FLOPS = 2 * 2 * BATCHES * KEYS * KEYS * C
@@ -35,12 +36,13 @@ def tile_qkvattention_pa_kernel(tc, q_scaled, k_scaled, v, out):
     with ExitStack() as ctx:
         keep = ctx.enter_context(tc.tile_pool(name="keep", bufs=1))
         scratch_pool = ctx.enter_context(tc.tile_pool(name="scratch", bufs=2))
-        quarter_pool = ctx.enter_context(tc.tile_pool(name="quarters", bufs=NORM_ROUNDS + 1))
+        quarter_pool = ctx.enter_context(tc.tile_pool(name="quarters", bufs=4))
+        v_pool = ctx.enter_context(tc.tile_pool(name="v_grouped", bufs=3))
         operand_pool = ctx.enter_context(tc.tile_pool(name="operands", bufs=2))
         dist_pool = ctx.enter_context(tc.tile_pool(name="distances", bufs=DIST_BUFS))
         weight_pool = ctx.enter_context(tc.tile_pool(name="weights", bufs=WEIGHT_BUFS))
-        mx_pool = ctx.enter_context(tc.tile_pool(name="mx", bufs=3))
-        code_pool = ctx.enter_context(tc.tile_pool(name="code", bufs=GROUP + 2))
+        mx_pool = ctx.enter_context(tc.tile_pool(name="mx", bufs=2))
+        code_pool = ctx.enter_context(tc.tile_pool(name="code", bufs=2))
         result_pool = ctx.enter_context(tc.tile_pool(name="results", bufs=3))
         score_psum = ctx.enter_context(tc.psum_pool(name="score_psum", bufs=4))
         weight_psum = ctx.enter_context(tc.psum_pool(name="weight_psum", bufs=2))
@@ -53,7 +55,6 @@ def tile_qkvattention_pa_kernel(tc, q_scaled, k_scaled, v, out):
         q_rows = keep.tile([P, BATCHES, TILES_PER_BATCH, C], BF16)
         k_rows = keep.tile([P, BATCHES, 2, 4, C], BF16)
         v_rows = keep.tile([P, BATCHES, PASSES, 4, C], BF16)
-        v_grouped = keep.tile([P, BATCHES, PASSES, C, 4], BF16, align_bytes=64)
         v_codes = keep.tile([P, BATCHES, PASSES * C], U32, align_bytes=64)
         v_scales = keep.tile([P, BATCHES, PASSES * C], U8, align_bytes=64)
         q2 = keep.tile([P, N_TILES], F32)
@@ -70,7 +71,7 @@ def tile_qkvattention_pa_kernel(tc, q_scaled, k_scaled, v, out):
 
         qT_of, kT_of, acc_of, dist_of, weight_of = {}, {}, {}, {}, {}
         wT_of, grouped_of, codes_of, scales_of, result_of = {}, {}, {}, {}, {}
-        partial_of, transposed_of = {}, {}
+        partial_of, transposed_of, v_grouped_of = {}, {}, {}
 
         def load_batch(b):
             k_view = k_scaled[b].rearrange("(a m u e) c -> u e m a c", a=4, m=64, u=2, e=2)
@@ -100,7 +101,10 @@ def tile_qkvattention_pa_kernel(tc, q_scaled, k_scaled, v, out):
                 return
             rows = norm_operands(n)[0]
             squares = scratch_pool.tile([P, TILES_PER_BATCH, C], F32, name="squares")
-            nc.scalar.activation(out=squares[:], in_=rows, func=FUNC.Square)
+            if n < SCALAR_SQUARES:
+                nc.scalar.activation(out=squares[:], in_=rows, func=FUNC.Square)
+            else:
+                nc.gpsimd.tensor_tensor(out=squares[:], in0=rows, in1=rows, op=ALU.mult)
             if n < 2:
                 partial_of[n] = squares
             else:
@@ -143,8 +147,9 @@ def tile_qkvattention_pa_kernel(tc, q_scaled, k_scaled, v, out):
         def regroup_v(b):
             if not 0 <= b < BATCHES:
                 return
+            v_grouped_of[b] = v_pool.tile([P, PASSES, C, 4], BF16, name="v_grouped", align_bytes=64)
             nc.gpsimd.tensor_scalar(
-                out=v_grouped[:, b],
+                out=v_grouped_of[b][:],
                 in0=v_rows[:, b].rearrange("p g j c -> p g c j"),
                 scalar1=1.0,
                 scalar2=0.0,
@@ -156,7 +161,7 @@ def tile_qkvattention_pa_kernel(tc, q_scaled, k_scaled, v, out):
             nc.vector.quantize_mx(
                 out=v_codes[:, b, :].bitcast(FP8X4),
                 scales=v_scales[:, b, :],
-                in_=v_grouped[:, b].rearrange("p g c j -> p (g c j)"),
+                in_=v_grouped_of[b][:].rearrange("p g c j -> p (g c j)"),
             )
 
         def scores(i):
@@ -236,18 +241,24 @@ def tile_qkvattention_pa_kernel(tc, q_scaled, k_scaled, v, out):
         def regroup(i):
             if not 0 <= i < N_TILES:
                 return
-            grouped_of[i] = mx_pool.tile([P, KEYS], BF16, name="grouped", align_bytes=64)
+            if i % GROUP == 0:
+                grouped_of[i // GROUP] = mx_pool.tile([P, GROUP, KEYS], BF16, name="grouped", align_bytes=64)
             nc.vector.tensor_copy(
-                out=grouped_of[i][:].bitcast(F32).rearrange("p (g t u) -> p g t u", g=PASSES, u=2),
+                out=grouped_of[i // GROUP][:, i % GROUP, :].bitcast(F32).rearrange("p (g t u) -> p g t u", g=PASSES, u=2),
                 in_=wT_of[i][:].rearrange("p (g u) t -> p g t u", g=PASSES),
             )
 
-        def quantise(i):
-            if not 0 <= i < N_TILES:
+        def quantise(last):
+            if not (0 <= last < N_TILES and last % GROUP == GROUP - 1):
                 return
-            codes_of[i] = code_pool.tile([P, PASSES * P], U32, name="codes", align_bytes=64)
-            scales_of[i] = code_pool.tile([P, PASSES * P], U8, name="scales", align_bytes=64)
-            nc.vector.quantize_mx(out=codes_of[i][:].bitcast(FP8X4), scales=scales_of[i][:], in_=grouped_of[i][:])
+            n = last // GROUP
+            codes_of[n] = code_pool.tile([P, GROUP * PASSES * P], U32, name="codes", align_bytes=64)
+            scales_of[n] = code_pool.tile([P, GROUP * PASSES * P], U8, name="scales", align_bytes=64)
+            nc.vector.quantize_mx(
+                out=codes_of[n][:].bitcast(FP8X4),
+                scales=scales_of[n][:],
+                in_=grouped_of[n][:].rearrange("p i k -> p (i k)"),
+            )
 
         def weighted_sums(last):
             if not (0 <= last < N_TILES and last % GROUP == GROUP - 1):
@@ -257,10 +268,11 @@ def tile_qkvattention_pa_kernel(tc, q_scaled, k_scaled, v, out):
             for i in range(last + 1 - GROUP, last + 1):
                 for g in range(PASSES):
                     cols = slice(g * P, (g + 1) * P)
+                    e_cols = slice((i % GROUP * PASSES + g) * P, (i % GROUP * PASSES + g + 1) * P)
                     nc.tensor.matmul_mx(
                         out=result_of[last // GROUP][:, i % GROUP, :],
-                        lhsT=codes_of[i][:, cols].bitcast(FP8X4),
-                        lhsT_scale=scales_of[i][:, cols],
+                        lhsT=codes_of[last // GROUP][:, e_cols].bitcast(FP8X4),
+                        lhsT_scale=scales_of[last // GROUP][:, e_cols],
                         rhs=v_codes[:, b, cols].bitcast(FP8X4),
                         rhs_scale=v_scales[:, b, cols],
                         start=(g == 0),
@@ -303,16 +315,27 @@ def tile_qkvattention_pa_kernel(tc, q_scaled, k_scaled, v, out):
         prepare(0, 2)
         finish_norms(1)
         scores(0)
+        pieces = []
+        for b in range(1, BATCHES):
+            pieces.extend([("norm", 2 * b), ("norm", 2 * b + 1)])
+            if b >= 2:
+                pieces.append(("v", b - 2))
+        pieces.extend([("v", BATCHES - 2), ("v", BATCHES - 1)])
         for r in range(N_TILES + LAG + 4):
             scores(r + 1)
             transpose_weights(r - LAG + 1)
             weighted_sums(r - LAG - 2)
             clamp_and_min(r)
             root(r)
-            start_norms(r + 2)
-            if r >= NORM_ROUNDS:
-                finish_norms(r + 2 - NORM_ROUNDS)
-            regroup_v(r + 2 - 2 * BATCHES)
+            if r < len(pieces):
+                kind, which = pieces[r]
+                if kind == "norm":
+                    start_norms(which)
+                else:
+                    regroup_v(which)
+            b, step = divmod(r + NORMS_AHEAD, TILES_PER_BATCH)
+            if 0 < b < BATCHES and step < 2:
+                finish_norms(2 * b + step)
             b, step = divmod(r + PREPARE_AHEAD, TILES_PER_BATCH)
             if 0 < b < BATCHES:
                 prepare(b, step)

@@ -24,7 +24,8 @@ PHASE = 16
 LAG = PHASE + 4
 DIST_BUFS = PHASE + 5
 WEIGHT_BUFS = 13
-SCALAR_SQUARES = 4
+SCALAR_SQUARES = 6
+EARLY_NORMS = 10
 NORMS_AHEAD = 6
 PREPARE_AHEAD = 4
 
@@ -68,6 +69,7 @@ def tile_qkvattention_pa_kernel(tc, q_scaled, k_scaled, v, out):
         inv_sum = keep.tile([P, N_TILES], F32)
         one = keep.tile([P, 1], F32)
         one_root = keep.tile([P, 1], F32)
+        held = keep.tile([P, N_TILES // GROUP], U32)
 
         qT_of, kT_of, acc_of, dist_of, weight_of = {}, {}, {}, {}, {}
         wT_of, grouped_of, codes_of, scales_of, result_of = {}, {}, {}, {}, {}
@@ -260,6 +262,16 @@ def tile_qkvattention_pa_kernel(tc, q_scaled, k_scaled, v, out):
                 in_=grouped_of[n][:].rearrange("p i k -> p (i k)"),
             )
 
+        def gpsimd_after_quantise(last):
+            if not (0 <= last < N_TILES and last % GROUP == GROUP - 1):
+                return
+            n = last // GROUP
+            if EARLY_NORMS + n >= 2 * BATCHES and n + 1 >= BATCHES:
+                return
+            nc.gpsimd.tensor_copy(out=held[:, n : n + 1], in_=codes_of[n][:, 0:1])
+            start_norms(EARLY_NORMS + n)
+            regroup_v(n + 1)
+
         def weighted_sums(last):
             if not (0 <= last < N_TILES and last % GROUP == GROUP - 1):
                 return
@@ -315,12 +327,7 @@ def tile_qkvattention_pa_kernel(tc, q_scaled, k_scaled, v, out):
         prepare(0, 2)
         finish_norms(1)
         scores(0)
-        pieces = []
-        for b in range(1, BATCHES):
-            pieces.extend([("norm", 2 * b), ("norm", 2 * b + 1)])
-            if b >= 2:
-                pieces.append(("v", b - 2))
-        pieces.extend([("v", BATCHES - 2), ("v", BATCHES - 1)])
+        pieces = [("norm", n) for n in range(2, EARLY_NORMS)] + [("v", 0)]
         for r in range(N_TILES + LAG + 4):
             scores(r + 1)
             transpose_weights(r - LAG + 1)
@@ -339,11 +346,12 @@ def tile_qkvattention_pa_kernel(tc, q_scaled, k_scaled, v, out):
             b, step = divmod(r + PREPARE_AHEAD, TILES_PER_BATCH)
             if 0 < b < BATCHES:
                 prepare(b, step)
-            b, step = divmod(r - (LAG - 2), TILES_PER_BATCH)
+            b, step = divmod(r - (LAG + 3), GROUP)
             if 0 <= b < BATCHES and step == 0:
                 quantise_v(b)
             regroup(r - LAG)
             quantise(r - LAG - 1)
+            gpsimd_after_quantise(r - LAG - 1)
             invert_sums(r - LAG - 2)
             divide_and_store(r - LAG - 3)
             if r % PHASE == PHASE - 1 and r < N_TILES:

@@ -59,10 +59,10 @@ def tile_qkvattention_pa_kernel(tc, q_scaled, k_scaled, v, out):
         v_codes = keep.tile([P, BATCHES, PASSES * C], U32, align_bytes=64)
         v_scales = keep.tile([P, BATCHES, PASSES * C], U8, align_bytes=64)
         q2 = keep.tile([P, N_TILES], F32)
-        neg_q2 = keep.tile([P, N_TILES], F32)
-        k2 = keep.tile([P, N_TILES], F32)
-        bank_min = keep.tile([P, N_TILES, 2], F32)
-        row_min = keep.tile([P, N_TILES], F32)
+        neg_k2 = keep.tile([P, N_TILES], F32)
+        first_k2 = keep.tile([P, TILES_PER_BATCH], F32)
+        bank_max = keep.tile([P, N_TILES, 2], F32)
+        row_max = keep.tile([P, N_TILES], F32)
         d2_min = keep.tile([P, N_TILES], F32)
         dist_min = keep.tile([P, N_TILES], F32)
         row_sum = keep.tile([P, N_TILES], F32)
@@ -73,7 +73,13 @@ def tile_qkvattention_pa_kernel(tc, q_scaled, k_scaled, v, out):
 
         qT_of, kT_of, acc_of, dist_of, weight_of = {}, {}, {}, {}, {}
         wT_of, grouped_of, codes_of, scales_of, result_of = {}, {}, {}, {}, {}
-        partial_of, transposed_of, v_grouped_of = {}, {}, {}
+        partial_of, transposed_of, transposed_k_of, v_grouped_of = {}, {}, {}, {}
+
+        def unit_start(i):
+            return i if i >= N_TILES - GROUP else i - i % GROUP
+
+        def ends_unit(i):
+            return 0 <= i < N_TILES and (i == N_TILES - 1 or unit_start(i + 1) == i + 1)
 
         def load_batch(b):
             k_view = k_scaled[b].rearrange("(a m u e) c -> u e m a c", a=4, m=64, u=2, e=2)
@@ -89,7 +95,7 @@ def tile_qkvattention_pa_kernel(tc, q_scaled, k_scaled, v, out):
             b = n // 2
             cols = slice(b * TILES_PER_BATCH, (b + 1) * TILES_PER_BATCH)
             if n % 2 == 0:
-                return k_rows[:, b].rearrange("p u a c -> p (u a) c"), k2[:, cols]
+                return k_rows[:, b].rearrange("p u a c -> p (u a) c"), neg_k2[:, cols]
             return q_rows[:, b], q2[:, cols]
 
         def fold(wide, pool, name):
@@ -103,48 +109,66 @@ def tile_qkvattention_pa_kernel(tc, q_scaled, k_scaled, v, out):
                 return
             rows = norm_operands(n)[0]
             squares = scratch_pool.tile([P, TILES_PER_BATCH, C], F32, name="squares")
+            if n < 2:
+                sums = first_k2[:] if n == 0 else norm_operands(n)[1]
+                for j in range(TILES_PER_BATCH):
+                    nc.scalar.activation(
+                        out=squares[:, j, :], in_=rows[:, j, :], func=FUNC.Square, accum_out=sums[:, j : j + 1]
+                    )
+                if n == 0:
+                    nc.scalar.mul(out=norm_operands(n)[1], in_=first_k2[:], mul=-1.0)
+                return
             if n < SCALAR_SQUARES:
                 nc.scalar.activation(out=squares[:], in_=rows, func=FUNC.Square)
             else:
                 nc.gpsimd.tensor_tensor(out=squares[:], in0=rows, in1=rows, op=ALU.mult)
-            if n < 2:
-                partial_of[n] = squares
-            else:
-                partial_of[n] = fold(fold(squares, scratch_pool, "halves"), quarter_pool, "quarters")
+            partial_of[n] = fold(fold(squares, scratch_pool, "halves"), quarter_pool, "quarters")
 
         def finish_norms(n):
             if not 0 <= n < 2 * BATCHES:
                 return
-            sums = norm_operands(n)[1]
-            nc.vector.tensor_reduce(out=sums, in_=partial_of[n][:], axis=AXIS_X, op=ALU.add)
-            if n % 2 == 1:
-                b = n // 2
-                cols = slice(b * TILES_PER_BATCH, (b + 1) * TILES_PER_BATCH)
-                nc.vector.tensor_scalar_mul(out=neg_q2[:, cols], in0=sums, scalar1=-1.0)
+            nc.vector.tensor_reduce(
+                out=norm_operands(n)[1], in_=partial_of[n][:], axis=AXIS_X, op=ALU.add, negate=(n % 2 == 0)
+            )
+
+        def transpose_q(b):
+            transposed_of[b] = operand_psum.tile([P, KEYS], BF16, name="transposed")
+            for j in range(TILES_PER_BATCH):
+                nc.tensor.transpose(
+                    out=transposed_of[b][:, j * P : (j + 1) * P], in_=q_rows[:, b, j, :], identity=ident_bf16[:]
+                )
+
+        def copy_q(b):
+            qT_of[b] = operand_pool.tile([P, KEYS], BF16, name="qT")
+            nc.vector.tensor_scalar_mul(out=qT_of[b][:], in0=transposed_of[b][:], scalar1=2.0)
+
+        def transpose_k(b):
+            if b == 0:
+                transposed_k_of[b] = weight_psum.tile([P, KEYS], BF16, name="wT")
+            else:
+                transposed_k_of[b] = operand_psum.tile([P, KEYS], BF16, name="transposed")
+            for g in range(PASSES):
+                for u in range(2):
+                    for h in range(2):
+                        col = 512 * g + 256 * u + 128 * h
+                        nc.tensor.transpose(
+                            out=transposed_k_of[b][:, col : col + P],
+                            in_=k_rows[:, b, u, 2 * g + h, :],
+                            identity=ident_bf16[:],
+                        )
+
+        def copy_k(b):
+            kT_of[b] = operand_pool.tile([P, KEYS], BF16, name="kT")
+            nc.vector.tensor_copy(out=kT_of[b][:], in_=transposed_k_of[b][:])
 
         def prepare(b, step):
             if step == 0:
-                transposed_of[b] = operand_psum.tile([P, KEYS], BF16, name="transposed")
-                for j in range(TILES_PER_BATCH):
-                    nc.tensor.transpose(
-                        out=transposed_of[b][:, j * P : (j + 1) * P], in_=q_rows[:, b, j, :], identity=ident_bf16[:]
-                    )
+                transpose_q(b)
             if step == 1:
-                qT_of[b] = operand_pool.tile([P, KEYS], BF16, name="qT")
-                nc.vector.tensor_scalar_mul(out=qT_of[b][:], in0=transposed_of[b][:], scalar1=-2.0)
-                transposed_of[b] = operand_psum.tile([P, KEYS], BF16, name="transposed")
-                for g in range(PASSES):
-                    for u in range(2):
-                        for h in range(2):
-                            col = 512 * g + 256 * u + 128 * h
-                            nc.tensor.transpose(
-                                out=transposed_of[b][:, col : col + P],
-                                in_=k_rows[:, b, u, 2 * g + h, :],
-                                identity=ident_bf16[:],
-                            )
+                copy_q(b)
+                transpose_k(b)
             if step == 2:
-                kT_of[b] = operand_pool.tile([P, KEYS], BF16, name="kT")
-                nc.vector.tensor_copy(out=kT_of[b][:], in_=transposed_of[b][:])
+                copy_k(b)
 
         def regroup_v(b):
             if not 0 <= b < BATCHES:
@@ -178,7 +202,7 @@ def tile_qkvattention_pa_kernel(tc, q_scaled, k_scaled, v, out):
                         block = b * TILES_PER_BATCH + 4 * u + 2 * g + h
                         nc.tensor.matmul(
                             out=acc[:, col : col + P],
-                            lhsT=k2[:, block : block + 1].to_broadcast([P, P]),
+                            lhsT=neg_k2[:, block : block + 1].to_broadcast([P, P]),
                             rhs=ident_f32[:],
                             is_transpose=True,
                             start=(col == 0),
@@ -201,24 +225,24 @@ def tile_qkvattention_pa_kernel(tc, q_scaled, k_scaled, v, out):
                 nc.vector.tensor_scalar(
                     out=dist_of[i][:, g * BANK : (g + 1) * BANK],
                     in0=acc_of[(i, g)][:],
-                    scalar1=neg_q2[:, i : i + 1],
+                    scalar1=q2[:, i : i + 1],
                     scalar2=None,
-                    op0=ALU.max,
-                    op1=ALU.min,
-                    accum_out=bank_min[:, i, g : g + 1],
+                    op0=ALU.min,
+                    op1=ALU.max,
+                    accum_out=bank_max[:, i, g : g + 1],
                 )
 
         def root(i):
             if not 0 <= i < N_TILES:
                 return
             nc.scalar.activation(
-                out=dist_of[i][:], in_=dist_of[i][:], func=FUNC.Sqrt, bias=q2[:, i : i + 1], scale=1.0
+                out=dist_of[i][:], in_=dist_of[i][:], func=FUNC.Sqrt, bias=q2[:, i : i + 1], scale=-1.0
             )
 
         def smallest_distances(first):
             cols = slice(first, first + PHASE)
-            nc.vector.tensor_reduce(out=row_min[:, cols], in_=bank_min[:, cols, :], axis=AXIS_X, op=ALU.min)
-            nc.vector.tensor_tensor(out=d2_min[:, cols], in0=row_min[:, cols], in1=q2[:, cols], op=ALU.add)
+            nc.vector.tensor_reduce(out=row_max[:, cols], in_=bank_max[:, cols, :], axis=AXIS_X, op=ALU.max)
+            nc.vector.tensor_tensor(out=d2_min[:, cols], in0=q2[:, cols], in1=row_max[:, cols], op=ALU.subtract)
             nc.scalar.activation(out=dist_min[:, cols], in_=d2_min[:, cols], func=FUNC.Sqrt)
 
         def weights(i):
@@ -243,48 +267,52 @@ def tile_qkvattention_pa_kernel(tc, q_scaled, k_scaled, v, out):
         def regroup(i):
             if not 0 <= i < N_TILES:
                 return
-            if i % GROUP == 0:
-                grouped_of[i // GROUP] = mx_pool.tile([P, GROUP, KEYS], BF16, name="grouped", align_bytes=64)
+            first = unit_start(i)
+            if i == first:
+                count = 1 if ends_unit(i) else GROUP
+                grouped_of[first] = mx_pool.tile([P, count, KEYS], BF16, name="grouped", align_bytes=64)
             nc.vector.tensor_copy(
-                out=grouped_of[i // GROUP][:, i % GROUP, :].bitcast(F32).rearrange("p (g t u) -> p g t u", g=PASSES, u=2),
+                out=grouped_of[first][:, i - first, :].bitcast(F32).rearrange("p (g t u) -> p g t u", g=PASSES, u=2),
                 in_=wT_of[i][:].rearrange("p (g u) t -> p g t u", g=PASSES),
             )
 
         def quantise(last):
-            if not (0 <= last < N_TILES and last % GROUP == GROUP - 1):
+            if not ends_unit(last):
                 return
-            n = last // GROUP
-            codes_of[n] = code_pool.tile([P, GROUP * PASSES * P], U32, name="codes", align_bytes=64)
-            scales_of[n] = code_pool.tile([P, GROUP * PASSES * P], U8, name="scales", align_bytes=64)
+            first = unit_start(last)
+            width = (last + 1 - first) * PASSES * P
+            codes_of[first] = code_pool.tile([P, width], U32, name="codes", align_bytes=64)
+            scales_of[first] = code_pool.tile([P, width], U8, name="scales", align_bytes=64)
             nc.vector.quantize_mx(
-                out=codes_of[n][:].bitcast(FP8X4),
-                scales=scales_of[n][:],
-                in_=grouped_of[n][:].rearrange("p i k -> p (i k)"),
+                out=codes_of[first][:].bitcast(FP8X4),
+                scales=scales_of[first][:],
+                in_=grouped_of[first][:].rearrange("p i k -> p (i k)"),
             )
 
         def gpsimd_after_quantise(last):
-            if not (0 <= last < N_TILES and last % GROUP == GROUP - 1):
+            if not ends_unit(last):
                 return
             n = last // GROUP
             if EARLY_NORMS + n >= 2 * BATCHES and n + 1 >= BATCHES:
                 return
-            nc.gpsimd.tensor_copy(out=held[:, n : n + 1], in_=codes_of[n][:, 0:1])
+            nc.gpsimd.tensor_copy(out=held[:, n : n + 1], in_=codes_of[unit_start(last)][:, 0:1])
             start_norms(EARLY_NORMS + n)
             regroup_v(n + 1)
 
         def weighted_sums(last):
-            if not (0 <= last < N_TILES and last % GROUP == GROUP - 1):
+            if not ends_unit(last):
                 return
+            first = unit_start(last)
             b = last // TILES_PER_BATCH
-            result_of[last // GROUP] = result_psum.tile([P, GROUP, C], F32, name="result")
-            for i in range(last + 1 - GROUP, last + 1):
+            result_of[first] = result_psum.tile([P, last + 1 - first, C], F32, name="result")
+            for i in range(first, last + 1):
                 for g in range(PASSES):
                     cols = slice(g * P, (g + 1) * P)
-                    e_cols = slice((i % GROUP * PASSES + g) * P, (i % GROUP * PASSES + g + 1) * P)
+                    e_cols = slice(((i - first) * PASSES + g) * P, ((i - first) * PASSES + g + 1) * P)
                     nc.tensor.matmul_mx(
-                        out=result_of[last // GROUP][:, i % GROUP, :],
-                        lhsT=codes_of[last // GROUP][:, e_cols].bitcast(FP8X4),
-                        lhsT_scale=scales_of[last // GROUP][:, e_cols],
+                        out=result_of[first][:, i - first, :],
+                        lhsT=codes_of[first][:, e_cols].bitcast(FP8X4),
+                        lhsT_scale=scales_of[first][:, e_cols],
                         rhs=v_codes[:, b, cols].bitcast(FP8X4),
                         rhs_scale=v_scales[:, b, cols],
                         start=(g == 0),
@@ -292,25 +320,26 @@ def tile_qkvattention_pa_kernel(tc, q_scaled, k_scaled, v, out):
                     )
 
         def invert_sums(last):
-            if not (0 <= last < N_TILES and last % GROUP == GROUP - 1):
+            if not ends_unit(last):
                 return
-            cols = slice(last + 1 - GROUP, last + 1)
+            cols = slice(unit_start(last), last + 1)
             nc.vector.reciprocal(out=inv_sum[:, cols], in_=row_sum[:, cols])
 
         def divide_and_store(last):
-            if not (0 <= last < N_TILES and last % GROUP == GROUP - 1):
+            if not ends_unit(last):
                 return
-            first = last + 1 - GROUP
+            first = unit_start(last)
+            count = last + 1 - first
             b, j = divmod(first, TILES_PER_BATCH)
-            final = result_pool.tile([P, GROUP, C], F32, name="final")
+            final = result_pool.tile([P, count, C], F32, name="final")
             nc.vector.tensor_tensor(
                 out=final[:],
-                in0=result_of[last // GROUP][:],
-                in1=inv_sum[:, first : last + 1].unsqueeze(2).to_broadcast([P, GROUP, C]),
+                in0=result_of[first][:],
+                in1=inv_sum[:, first : last + 1].unsqueeze(2).to_broadcast([P, count, C]),
                 op=ALU.mult,
             )
             rows = out[b].rearrange("(p j) c -> p j c", j=TILES_PER_BATCH)
-            nc.sync.dma_start(out=rows[:, j : j + GROUP, :], in_=final[:])
+            nc.sync.dma_start(out=rows[:, j : j + count, :], in_=final[:])
 
         for b in range(BATCHES):
             load_batch(b)
@@ -321,11 +350,10 @@ def tile_qkvattention_pa_kernel(tc, q_scaled, k_scaled, v, out):
 
         start_norms(0)
         start_norms(1)
-        prepare(0, 0)
-        prepare(0, 1)
-        finish_norms(0)
-        prepare(0, 2)
-        finish_norms(1)
+        transpose_k(0)
+        transpose_q(0)
+        copy_k(0)
+        copy_q(0)
         scores(0)
         pieces = [("norm", n) for n in range(2, EARLY_NORMS)] + [("v", 0)]
         for r in range(N_TILES + LAG + 4):

@@ -26,7 +26,7 @@ DIST_BUFS = PHASE + 5
 WEIGHT_BUFS = 13
 SCALAR_SQUARES = 6
 EARLY_NORMS = 10
-NORMS_AHEAD = 6
+NORMS_AHEAD = 3
 PREPARE_AHEAD = 4
 
 FLOPS = 2 * 2 * BATCHES * KEYS * KEYS * C
@@ -37,7 +37,7 @@ def tile_qkvattention_pa_kernel(tc, q_scaled, k_scaled, v, out):
     with ExitStack() as ctx:
         keep = ctx.enter_context(tc.tile_pool(name="keep", bufs=1))
         scratch_pool = ctx.enter_context(tc.tile_pool(name="scratch", bufs=2))
-        quarter_pool = ctx.enter_context(tc.tile_pool(name="quarters", bufs=4))
+        folded_pool = ctx.enter_context(tc.tile_pool(name="folded", bufs=4))
         v_pool = ctx.enter_context(tc.tile_pool(name="v_grouped", bufs=3))
         operand_pool = ctx.enter_context(tc.tile_pool(name="operands", bufs=2))
         dist_pool = ctx.enter_context(tc.tile_pool(name="distances", bufs=DIST_BUFS))
@@ -122,7 +122,8 @@ def tile_qkvattention_pa_kernel(tc, q_scaled, k_scaled, v, out):
                 nc.scalar.activation(out=squares[:], in_=rows, func=FUNC.Square)
             else:
                 nc.gpsimd.tensor_tensor(out=squares[:], in0=rows, in1=rows, op=ALU.mult)
-            partial_of[n] = fold(fold(squares, scratch_pool, "halves"), quarter_pool, "quarters")
+            eighths = fold(fold(fold(squares, scratch_pool, "halves"), scratch_pool, "quarters"), scratch_pool, "eighths")
+            partial_of[n] = fold(eighths, folded_pool, "sixteenths")
 
         def finish_norms(n):
             if not 0 <= n < 2 * BATCHES:
@@ -374,10 +375,10 @@ def tile_qkvattention_pa_kernel(tc, q_scaled, k_scaled, v, out):
             b, step = divmod(r + PREPARE_AHEAD, TILES_PER_BATCH)
             if 0 < b < BATCHES:
                 prepare(b, step)
-            b, step = divmod(r - (LAG + 3), GROUP)
+            regroup(r - LAG)
+            b, step = divmod(r - (LAG + GROUP), GROUP)
             if 0 <= b < BATCHES and step == 0:
                 quantise_v(b)
-            regroup(r - LAG)
             quantise(r - LAG - 1)
             gpsimd_after_quantise(r - LAG - 1)
             invert_sums(r - LAG - 2)

@@ -27,6 +27,7 @@ WEIGHT_BUFS = 13
 SCALAR_SQUARES = 6
 EARLY_NORMS = 10
 NORMS_AHEAD = 3
+SCALAR_DIVIDES = 8
 PREPARE_AHEAD = 4
 
 FLOPS = 2 * 2 * BATCHES * KEYS * KEYS * C
@@ -333,12 +334,21 @@ def tile_qkvattention_pa_kernel(tc, q_scaled, k_scaled, v, out):
             count = last + 1 - first
             b, j = divmod(first, TILES_PER_BATCH)
             final = result_pool.tile([P, count, C], F32, name="final")
-            nc.vector.tensor_tensor(
-                out=final[:],
-                in0=result_of[first][:],
-                in1=inv_sum[:, first : last + 1].unsqueeze(2).to_broadcast([P, count, C]),
-                op=ALU.mult,
-            )
+            if first >= N_TILES - SCALAR_DIVIDES:
+                for i in range(first, last + 1):
+                    nc.scalar.activation(
+                        out=final[:, i - first, :],
+                        in_=result_of[first][:, i - first, :],
+                        func=FUNC.Copy,
+                        scale=inv_sum[:, i : i + 1],
+                    )
+            else:
+                nc.vector.tensor_tensor(
+                    out=final[:],
+                    in0=result_of[first][:],
+                    in1=inv_sum[:, first : last + 1].unsqueeze(2).to_broadcast([P, count, C]),
+                    op=ALU.mult,
+                )
             rows = out[b].rearrange("(p j) c -> p j c", j=TILES_PER_BATCH)
             nc.sync.dma_start(out=rows[:, j : j + count, :], in_=final[:])
 

@@ -26,7 +26,7 @@ DIST_BUFS = PHASE + 5
 WEIGHT_BUFS = 13
 SCALAR_SQUARES = 6
 EARLY_NORMS = 10
-NORMS_AHEAD = 3
+NORMS_AHEAD = 2
 SCALAR_DIVIDES = 8
 PREPARE_AHEAD = 4
 

@@ -20,12 +20,11 @@ TILES_PER_BATCH = KEYS // P
 N_TILES = BATCHES * TILES_PER_BATCH
 GROUP = 4
 
-PHASE = 16
-LAG = PHASE + 4
-DIST_BUFS = PHASE + 5
-WEIGHT_BUFS = 13
+PHASES = (16, 24, 24)
+LAG = max(PHASES) + 4
+DIST_BUFS = LAG + 2
 SCALAR_SQUARES = 6
-EARLY_NORMS = 10
+EARLY_NORMS = 12
 NORMS_AHEAD = 2
 SCALAR_DIVIDES = 8
 PREPARE_AHEAD = 4
@@ -38,14 +37,13 @@ def tile_qkvattention_pa_kernel(tc, q_scaled, k_scaled, v, out):
     with ExitStack() as ctx:
         keep = ctx.enter_context(tc.tile_pool(name="keep", bufs=1))
         scratch_pool = ctx.enter_context(tc.tile_pool(name="scratch", bufs=2))
-        folded_pool = ctx.enter_context(tc.tile_pool(name="folded", bufs=4))
-        v_pool = ctx.enter_context(tc.tile_pool(name="v_grouped", bufs=3))
+        folded_pool = ctx.enter_context(tc.tile_pool(name="folded", bufs=6))
+        v_pool = ctx.enter_context(tc.tile_pool(name="v_grouped", bufs=2))
         operand_pool = ctx.enter_context(tc.tile_pool(name="operands", bufs=2))
         dist_pool = ctx.enter_context(tc.tile_pool(name="distances", bufs=DIST_BUFS))
-        weight_pool = ctx.enter_context(tc.tile_pool(name="weights", bufs=WEIGHT_BUFS))
         mx_pool = ctx.enter_context(tc.tile_pool(name="mx", bufs=2))
         code_pool = ctx.enter_context(tc.tile_pool(name="code", bufs=2))
-        result_pool = ctx.enter_context(tc.tile_pool(name="results", bufs=3))
+        result_pool = ctx.enter_context(tc.tile_pool(name="results", bufs=2))
         score_psum = ctx.enter_context(tc.psum_pool(name="score_psum", bufs=4))
         weight_psum = ctx.enter_context(tc.psum_pool(name="weight_psum", bufs=2))
         result_psum = ctx.enter_context(tc.psum_pool(name="result_psum", bufs=1))
@@ -72,7 +70,7 @@ def tile_qkvattention_pa_kernel(tc, q_scaled, k_scaled, v, out):
         one_root = keep.tile([P, 1], F32)
         held = keep.tile([P, N_TILES // GROUP], U32)
 
-        qT_of, kT_of, acc_of, dist_of, weight_of = {}, {}, {}, {}, {}
+        qT_of, kT_of, acc_of, dist_of = {}, {}, {}, {}
         wT_of, grouped_of, codes_of, scales_of, result_of = {}, {}, {}, {}, {}
         partial_of, transposed_of, transposed_k_of, v_grouped_of = {}, {}, {}, {}
 
@@ -241,16 +239,15 @@ def tile_qkvattention_pa_kernel(tc, q_scaled, k_scaled, v, out):
                 out=dist_of[i][:], in_=dist_of[i][:], func=FUNC.Sqrt, bias=q2[:, i : i + 1], scale=-1.0
             )
 
-        def smallest_distances(first):
-            cols = slice(first, first + PHASE)
+        def smallest_distances(first, count):
+            cols = slice(first, first + count)
             nc.vector.tensor_reduce(out=row_max[:, cols], in_=bank_max[:, cols, :], axis=AXIS_X, op=ALU.max)
             nc.vector.tensor_tensor(out=d2_min[:, cols], in0=q2[:, cols], in1=row_max[:, cols], op=ALU.subtract)
             nc.scalar.activation(out=dist_min[:, cols], in_=d2_min[:, cols], func=FUNC.Sqrt)
 
         def weights(i):
-            weight_of[i] = weight_pool.tile([P, KEYS], BF16, name="weight")
             nc.scalar.activation(
-                out=weight_of[i][:],
+                out=dist_of[i][:].bitcast(BF16)[:, 0:KEYS],
                 in_=dist_of[i][:],
                 func=FUNC.Exp,
                 bias=dist_min[:, i : i + 1],
@@ -261,7 +258,7 @@ def tile_qkvattention_pa_kernel(tc, q_scaled, k_scaled, v, out):
         def transpose_weights(i):
             if not 0 <= i < N_TILES:
                 return
-            words = weight_of[i][:].bitcast(F32)
+            words = dist_of[i][:, 0 : KEYS // 2]
             wT_of[i] = weight_psum.tile([P, 2 * PASSES, P], F32, name="wT")
             for n in range(2 * PASSES):
                 nc.tensor.transpose(out=wT_of[i][:, n, :], in_=words[:, n * P : (n + 1) * P], identity=ident_f32[:])
@@ -352,6 +349,9 @@ def tile_qkvattention_pa_kernel(tc, q_scaled, k_scaled, v, out):
             rows = out[b].rearrange("(p j) c -> p j c", j=TILES_PER_BATCH)
             nc.sync.dma_start(out=rows[:, j : j + count, :], in_=final[:])
 
+        phase_ending_at = {}
+        for n, count in enumerate(PHASES):
+            phase_ending_at[sum(PHASES[: n + 1]) - 1] = (sum(PHASES[:n]), count)
         for b in range(BATCHES):
             load_batch(b)
         make_identity(nc, ident_bf16[:])
@@ -393,8 +393,8 @@ def tile_qkvattention_pa_kernel(tc, q_scaled, k_scaled, v, out):
             gpsimd_after_quantise(r - LAG - 1)
             invert_sums(r - LAG - 2)
             divide_and_store(r - LAG - 3)
-            if r % PHASE == PHASE - 1 and r < N_TILES:
-                first = r + 1 - PHASE
-                smallest_distances(first)
-                for i in range(first, first + PHASE):
+            if r in phase_ending_at:
+                first, count = phase_ending_at[r]
+                smallest_distances(first, count)
+                for i in range(first, first + count):
                     weights(i)

@@ -22,7 +22,7 @@ GROUP = 4
 
 PHASES = (16, 24, 24)
 LAG = max(PHASES) + 4
-DIST_BUFS = LAG + 2
+DIST_BUFS = LAG + 1
 SCALAR_SQUARES = 6
 EARLY_NORMS = 12
 NORMS_AHEAD = 2
@@ -57,10 +57,10 @@ def tile_qkvattention_pa_kernel(tc, q_scaled, k_scaled, v, out):
         v_rows = keep.tile([P, BATCHES, PASSES, 4, C], BF16)
         v_codes = keep.tile([P, BATCHES, PASSES * C], U32, align_bytes=64)
         v_scales = keep.tile([P, BATCHES, PASSES * C], U8, align_bytes=64)
-        q2 = keep.tile([P, N_TILES], F32)
+        peaks = keep.tile([P, N_TILES, 3], F32)
+        raised_q2 = keep.tile([P, N_TILES], F32)
         neg_k2 = keep.tile([P, N_TILES], F32)
         first_k2 = keep.tile([P, TILES_PER_BATCH], F32)
-        bank_max = keep.tile([P, N_TILES, 2], F32)
         row_max = keep.tile([P, N_TILES], F32)
         d2_min = keep.tile([P, N_TILES], F32)
         dist_min = keep.tile([P, N_TILES], F32)
@@ -95,7 +95,7 @@ def tile_qkvattention_pa_kernel(tc, q_scaled, k_scaled, v, out):
             cols = slice(b * TILES_PER_BATCH, (b + 1) * TILES_PER_BATCH)
             if n % 2 == 0:
                 return k_rows[:, b].rearrange("p u a c -> p (u a) c"), neg_k2[:, cols]
-            return q_rows[:, b], q2[:, cols]
+            return q_rows[:, b], peaks[:, cols, 2]
 
         def fold(wide, pool, name):
             width = wide.shape[2] // 2
@@ -225,24 +225,30 @@ def tile_qkvattention_pa_kernel(tc, q_scaled, k_scaled, v, out):
                 nc.vector.tensor_scalar(
                     out=dist_of[i][:, g * BANK : (g + 1) * BANK],
                     in0=acc_of[(i, g)][:],
-                    scalar1=q2[:, i : i + 1],
+                    scalar1=1.0,
                     scalar2=None,
-                    op0=ALU.min,
+                    op0=ALU.mult,
                     op1=ALU.max,
-                    accum_out=bank_max[:, i, g : g + 1],
+                    accum_out=peaks[:, i, g : g + 1],
                 )
+
+        def raise_q2(last):
+            if last not in group_ending_at:
+                return
+            cols = slice(group_ending_at[last], last + 1)
+            nc.vector.tensor_reduce(out=raised_q2[:, cols], in_=peaks[:, cols, :], axis=AXIS_X, op=ALU.max)
 
         def root(i):
             if not 0 <= i < N_TILES:
                 return
             nc.scalar.activation(
-                out=dist_of[i][:], in_=dist_of[i][:], func=FUNC.Sqrt, bias=q2[:, i : i + 1], scale=-1.0
+                out=dist_of[i][:], in_=dist_of[i][:], func=FUNC.Sqrt, bias=raised_q2[:, i : i + 1], scale=-1.0
             )
 
         def smallest_distances(first, count):
             cols = slice(first, first + count)
-            nc.vector.tensor_reduce(out=row_max[:, cols], in_=bank_max[:, cols, :], axis=AXIS_X, op=ALU.max)
-            nc.vector.tensor_tensor(out=d2_min[:, cols], in0=q2[:, cols], in1=row_max[:, cols], op=ALU.subtract)
+            nc.vector.tensor_reduce(out=row_max[:, cols], in_=peaks[:, cols, 0:2], axis=AXIS_X, op=ALU.max)
+            nc.vector.tensor_tensor(out=d2_min[:, cols], in0=raised_q2[:, cols], in1=row_max[:, cols], op=ALU.subtract)
             nc.scalar.activation(out=dist_min[:, cols], in_=d2_min[:, cols], func=FUNC.Sqrt)
 
         def weights(i):
@@ -352,6 +358,14 @@ def tile_qkvattention_pa_kernel(tc, q_scaled, k_scaled, v, out):
         phase_ending_at = {}
         for n, count in enumerate(PHASES):
             phase_ending_at[sum(PHASES[: n + 1]) - 1] = (sum(PHASES[:n]), count)
+        group_ending_at = {}
+        for last_of_phase in phase_ending_at:
+            first_of_phase, count = phase_ending_at[last_of_phase]
+            end = last_of_phase
+            for size in [1, 1, 2] + [4] * ((count - 4) // 4):
+                group_ending_at[end] = end - size + 1
+                end -= size
+            assert end == first_of_phase - 1
         for b in range(BATCHES):
             load_batch(b)
         make_identity(nc, ident_bf16[:])
@@ -372,7 +386,10 @@ def tile_qkvattention_pa_kernel(tc, q_scaled, k_scaled, v, out):
             transpose_weights(r - LAG + 1)
             weighted_sums(r - LAG - 2)
             clamp_and_min(r)
-            root(r)
+            raise_q2(r)
+            if r in group_ending_at:
+                for i in range(group_ending_at[r], r + 1):
+                    root(i)
             if r < len(pieces):
                 kind, which = pieces[r]
                 if kind == "norm":

@@ -43,7 +43,7 @@ def tile_qkvattention_pa_kernel(tc, q_scaled, k_scaled, v, out):
         dist_pool = ctx.enter_context(tc.tile_pool(name="distances", bufs=DIST_BUFS))
         mx_pool = ctx.enter_context(tc.tile_pool(name="mx", bufs=2))
         code_pool = ctx.enter_context(tc.tile_pool(name="code", bufs=2))
-        result_pool = ctx.enter_context(tc.tile_pool(name="results", bufs=2))
+        result_pool = ctx.enter_context(tc.tile_pool(name="results", bufs=3))
         score_psum = ctx.enter_context(tc.psum_pool(name="score_psum", bufs=4))
         weight_psum = ctx.enter_context(tc.psum_pool(name="weight_psum", bufs=2))
         result_psum = ctx.enter_context(tc.psum_pool(name="result_psum", bufs=1))
@@ -309,7 +309,10 @@ def tile_qkvattention_pa_kernel(tc, q_scaled, k_scaled, v, out):
                 return
             first = unit_start(last)
             b = last // TILES_PER_BATCH
-            result_of[first] = result_psum.tile([P, last + 1 - first, C], F32, name="result")
+            if first >= N_TILES - SCALAR_DIVIDES:
+                result_of[first] = score_psum.tile([P, last + 1 - first, C], F32, name="acc")
+            else:
+                result_of[first] = result_psum.tile([P, last + 1 - first, C], F32, name="result")
             for i in range(first, last + 1):
                 for g in range(PASSES):
                     cols = slice(g * P, (g + 1) * P)
@@ -327,7 +330,12 @@ def tile_qkvattention_pa_kernel(tc, q_scaled, k_scaled, v, out):
         def invert_sums(last):
             if not ends_unit(last):
                 return
-            cols = slice(unit_start(last), last + 1)
+            first = unit_start(last)
+            if first < N_TILES - TILES_PER_BATCH:
+                if first % TILES_PER_BATCH != 0:
+                    return
+                last = first + TILES_PER_BATCH - 1
+            cols = slice(first, last + 1)
             nc.vector.reciprocal(out=inv_sum[:, cols], in_=row_sum[:, cols])
 
         def divide_and_store(last):
@@ -336,7 +344,7 @@ def tile_qkvattention_pa_kernel(tc, q_scaled, k_scaled, v, out):
             first = unit_start(last)
             count = last + 1 - first
             b, j = divmod(first, TILES_PER_BATCH)
-            final = result_pool.tile([P, count, C], F32, name="final")
+            final = result_pool.tile([P, count, C], F32, name="final" if count == GROUP else "final_of_one")
             if first >= N_TILES - SCALAR_DIVIDES:
                 for i in range(first, last + 1):
                     nc.scalar.activation(
@@ -362,7 +370,7 @@ def tile_qkvattention_pa_kernel(tc, q_scaled, k_scaled, v, out):
         for last_of_phase in phase_ending_at:
             first_of_phase, count = phase_ending_at[last_of_phase]
             end = last_of_phase
-            for size in [1, 1, 2] + [4] * ((count - 4) // 4):
+            for size in [1, 1, 2, 4] + ([4, 4] if first_of_phase == 0 else [8] * ((count - 8) // 8)):
                 group_ending_at[end] = end - size + 1
                 end -= size
             assert end == first_of_phase - 1
@@ -380,7 +388,7 @@ def tile_qkvattention_pa_kernel(tc, q_scaled, k_scaled, v, out):
         copy_k(0)
         copy_q(0)
         scores(0)
-        pieces = [("norm", n) for n in range(2, EARLY_NORMS)] + [("v", 0)]
+        pieces = [("norm", n) for n in range(2, 8)] + [("v", 0)] + [("norm", n) for n in range(8, EARLY_NORMS)]
         for r in range(N_TILES + LAG + 4):
             scores(r + 1)
             transpose_weights(r - LAG + 1)

from contextlib import ExitStack

import concourse.mybir as mybir
from concourse.masks import make_identity

F32 = mybir.dt.float32
BF16 = mybir.dt.bfloat16
U32 = mybir.dt.uint32
U8 = mybir.dt.uint8
FP8X4 = mybir.dt.float8_e4m3fn_x4
ALU = mybir.AluOpType
FUNC = mybir.ActivationFunctionType
AXIS_X = mybir.AxisListType.X

P = 128
BATCHES, KEYS, C = 8, 1024, 128
BANK = 512
PASSES = KEYS // (4 * P)
TILES_PER_BATCH = KEYS // P
N_TILES = BATCHES * TILES_PER_BATCH
GROUP = 4

PHASES = (16, 24, 24)
LAG = max(PHASES) + 4
DIST_BUFS = LAG + 1
SCALAR_SQUARES = 6
EARLY_NORMS = 12
NORMS_AHEAD = 2
SCALAR_DIVIDES = 8
PREPARE_AHEAD = 4

FLOPS = 2 * 2 * BATCHES * KEYS * KEYS * C


def tile_qkvattention_pa_kernel(tc, q_scaled, k_scaled, v, out):
    nc = tc.nc
    with ExitStack() as ctx:
        keep = ctx.enter_context(tc.tile_pool(name="keep", bufs=1))
        scratch_pool = ctx.enter_context(tc.tile_pool(name="scratch", bufs=2))
        folded_pool = ctx.enter_context(tc.tile_pool(name="folded", bufs=6))
        v_pool = ctx.enter_context(tc.tile_pool(name="v_grouped", bufs=2))
        operand_pool = ctx.enter_context(tc.tile_pool(name="operands", bufs=2))
        dist_pool = ctx.enter_context(tc.tile_pool(name="distances", bufs=DIST_BUFS))
        mx_pool = ctx.enter_context(tc.tile_pool(name="mx", bufs=2))
        code_pool = ctx.enter_context(tc.tile_pool(name="code", bufs=2))
        result_pool = ctx.enter_context(tc.tile_pool(name="results", bufs=3))
        score_psum = ctx.enter_context(tc.psum_pool(name="score_psum", bufs=4))
        weight_psum = ctx.enter_context(tc.psum_pool(name="weight_psum", bufs=2))
        result_psum = ctx.enter_context(tc.psum_pool(name="result_psum", bufs=1))
        operand_psum = ctx.enter_context(tc.psum_pool(name="operand_psum", bufs=1))
        ctx.enter_context(tc.manual_schedule())

        ident_bf16 = keep.tile([P, P], BF16)
        ident_f32 = keep.tile([P, P], F32)
        q_rows = keep.tile([P, BATCHES, TILES_PER_BATCH, C], BF16)
        k_rows = keep.tile([P, BATCHES, 2, 4, C], BF16)
        v_rows = keep.tile([P, BATCHES, PASSES, 4, C], BF16)
        v_codes = keep.tile([P, BATCHES, PASSES * C], U32, align_bytes=64)
        v_scales = keep.tile([P, BATCHES, PASSES * C], U8, align_bytes=64)
        peaks = keep.tile([P, N_TILES, 3], F32)
        raised_q2 = keep.tile([P, N_TILES], F32)
        neg_k2 = keep.tile([P, N_TILES], F32)
        first_k2 = keep.tile([P, TILES_PER_BATCH], F32)
        row_max = keep.tile([P, N_TILES], F32)
        d2_min = keep.tile([P, N_TILES], F32)
        dist_min = keep.tile([P, N_TILES], F32)
        row_sum = keep.tile([P, N_TILES], F32)
        inv_sum = keep.tile([P, N_TILES], F32)
        one = keep.tile([P, 1], F32)
        one_root = keep.tile([P, 1], F32)
        held = keep.tile([P, N_TILES // GROUP], U32)

        qT_of, kT_of, acc_of, dist_of = {}, {}, {}, {}
        wT_of, grouped_of, codes_of, scales_of, result_of = {}, {}, {}, {}, {}
        partial_of, transposed_of, transposed_k_of, v_grouped_of = {}, {}, {}, {}

        def unit_start(i):
            return i if i >= N_TILES - GROUP else i - i % GROUP

        def ends_unit(i):
            return 0 <= i < N_TILES and (i == N_TILES - 1 or unit_start(i + 1) == i + 1)

        def load_batch(b):
            k_view = k_scaled[b].rearrange("(a m u e) c -> u e m a c", a=4, m=64, u=2, e=2)
            for u in range(2):
                for e in range(2):
                    nc.sync.dma_start(out=k_rows[e:P:2, b, u, :, :], in_=k_view[u, e])
            nc.sync.dma_start(
                out=q_rows[:, b], in_=q_scaled[b].rearrange("(p j) c -> p j c", j=TILES_PER_BATCH)
            )
            nc.sync.dma_start(out=v_rows[:, b], in_=v[b].rearrange("(g p j) c -> p g j c", g=PASSES, j=4))

        def norm_operands(n):
            b = n // 2
            cols = slice(b * TILES_PER_BATCH, (b + 1) * TILES_PER_BATCH)
            if n % 2 == 0:
                return k_rows[:, b].rearrange("p u a c -> p (u a) c"), neg_k2[:, cols]
            return q_rows[:, b], peaks[:, cols, 2]

        def fold(wide, pool, name):
            width = wide.shape[2] // 2
            narrow = pool.tile([P, TILES_PER_BATCH, width], F32, name=name)
            nc.gpsimd.tensor_tensor(out=narrow[:], in0=wide[:, :, :width], in1=wide[:, :, width:], op=ALU.add)
            return narrow

        def start_norms(n):
            if not 0 <= n < 2 * BATCHES:
                return
            rows = norm_operands(n)[0]
            squares = scratch_pool.tile([P, TILES_PER_BATCH, C], F32, name="squares")
            if n < 2:
                sums = first_k2[:] if n == 0 else norm_operands(n)[1]
                for j in range(TILES_PER_BATCH):
                    nc.scalar.activation(
                        out=squares[:, j, :], in_=rows[:, j, :], func=FUNC.Square, accum_out=sums[:, j : j + 1]
                    )
                if n == 0:
                    nc.scalar.mul(out=norm_operands(n)[1], in_=first_k2[:], mul=-1.0)
                return
            if n < SCALAR_SQUARES:
                nc.scalar.activation(out=squares[:], in_=rows, func=FUNC.Square)
            else:
                nc.gpsimd.tensor_tensor(out=squares[:], in0=rows, in1=rows, op=ALU.mult)
            eighths = fold(fold(fold(squares, scratch_pool, "halves"), scratch_pool, "quarters"), scratch_pool, "eighths")
            partial_of[n] = fold(eighths, folded_pool, "sixteenths")

        def finish_norms(n):
            if not 0 <= n < 2 * BATCHES:
                return
            nc.vector.tensor_reduce(
                out=norm_operands(n)[1], in_=partial_of[n][:], axis=AXIS_X, op=ALU.add, negate=(n % 2 == 0)
            )

        def transpose_q(b):
            transposed_of[b] = operand_psum.tile([P, KEYS], BF16, name="transposed")
            for j in range(TILES_PER_BATCH):
                nc.tensor.transpose(
                    out=transposed_of[b][:, j * P : (j + 1) * P], in_=q_rows[:, b, j, :], identity=ident_bf16[:]
                )

        def copy_q(b):
            qT_of[b] = operand_pool.tile([P, KEYS], BF16, name="qT")
            nc.vector.tensor_scalar_mul(out=qT_of[b][:], in0=transposed_of[b][:], scalar1=2.0)

        def transpose_k(b):
            if b == 0:
                transposed_k_of[b] = weight_psum.tile([P, KEYS], BF16, name="wT")
            else:
                transposed_k_of[b] = operand_psum.tile([P, KEYS], BF16, name="transposed")
            for g in range(PASSES):
                for u in range(2):
                    for h in range(2):
                        col = 512 * g + 256 * u + 128 * h
                        nc.tensor.transpose(
                            out=transposed_k_of[b][:, col : col + P],
                            in_=k_rows[:, b, u, 2 * g + h, :],
                            identity=ident_bf16[:],
                        )

        def copy_k(b):
            kT_of[b] = operand_pool.tile([P, KEYS], BF16, name="kT")
            nc.vector.tensor_copy(out=kT_of[b][:], in_=transposed_k_of[b][:])

        def prepare(b, step):
            if step == 0:
                transpose_q(b)
            if step == 1:
                copy_q(b)
                transpose_k(b)
            if step == 2:
                copy_k(b)

        def regroup_v(b):
            if not 0 <= b < BATCHES:
                return
            v_grouped_of[b] = v_pool.tile([P, PASSES, C, 4], BF16, name="v_grouped", align_bytes=64)
            nc.gpsimd.tensor_scalar(
                out=v_grouped_of[b][:],
                in0=v_rows[:, b].rearrange("p g j c -> p g c j"),
                scalar1=1.0,
                scalar2=0.0,
                op0=ALU.mult,
                op1=ALU.add,
            )

        def quantise_v(b):
            nc.vector.quantize_mx(
                out=v_codes[:, b, :].bitcast(FP8X4),
                scales=v_scales[:, b, :],
                in_=v_grouped_of[b][:].rearrange("p g c j -> p (g c j)"),
            )

        def scores(i):
            if not 0 <= i < N_TILES:
                return
            b, j = divmod(i, TILES_PER_BATCH)
            for g in range(PASSES):
                acc = score_psum.tile([P, BANK], F32, name="acc")
                for u in range(2):
                    for h in range(2):
                        col = 256 * u + 128 * h
                        block = b * TILES_PER_BATCH + 4 * u + 2 * g + h
                        nc.tensor.matmul(
                            out=acc[:, col : col + P],
                            lhsT=neg_k2[:, block : block + 1].to_broadcast([P, P]),
                            rhs=ident_f32[:],
                            is_transpose=True,
                            start=(col == 0),
                            stop=False,
                        )
                nc.tensor.matmul(
                    out=acc[:],
                    lhsT=qT_of[b][:, j * P : (j + 1) * P],
                    rhs=kT_of[b][:, g * BANK : (g + 1) * BANK],
                    start=False,
                    stop=True,
                )
                acc_of[(i, g)] = acc

        def clamp_and_min(i):
            if not 0 <= i < N_TILES:
                return
            dist_of[i] = dist_pool.tile([P, KEYS], F32, name="dist")
            for g in range(PASSES):
                nc.vector.tensor_scalar(
                    out=dist_of[i][:, g * BANK : (g + 1) * BANK],
                    in0=acc_of[(i, g)][:],
                    scalar1=1.0,
                    scalar2=None,
                    op0=ALU.mult,
                    op1=ALU.max,
                    accum_out=peaks[:, i, g : g + 1],
                )

        def raise_q2(last):
            if last not in group_ending_at:
                return
            cols = slice(group_ending_at[last], last + 1)
            nc.vector.tensor_reduce(out=raised_q2[:, cols], in_=peaks[:, cols, :], axis=AXIS_X, op=ALU.max)

        def root(i):
            if not 0 <= i < N_TILES:
                return
            nc.scalar.activation(
                out=dist_of[i][:], in_=dist_of[i][:], func=FUNC.Sqrt, bias=raised_q2[:, i : i + 1], scale=-1.0
            )

        def smallest_distances(first, count):
            cols = slice(first, first + count)
            nc.vector.tensor_reduce(out=row_max[:, cols], in_=peaks[:, cols, 0:2], axis=AXIS_X, op=ALU.max)
            nc.vector.tensor_tensor(out=d2_min[:, cols], in0=raised_q2[:, cols], in1=row_max[:, cols], op=ALU.subtract)
            nc.scalar.activation(out=dist_min[:, cols], in_=d2_min[:, cols], func=FUNC.Sqrt)

        def weights(i):
            nc.scalar.activation(
                out=dist_of[i][:].bitcast(BF16)[:, 0:KEYS],
                in_=dist_of[i][:],
                func=FUNC.Exp,
                bias=dist_min[:, i : i + 1],
                scale=-1.0,
                accum_out=row_sum[:, i : i + 1],
            )

        def transpose_weights(i):
            if not 0 <= i < N_TILES:
                return
            words = dist_of[i][:, 0 : KEYS // 2]
            wT_of[i] = weight_psum.tile([P, 2 * PASSES, P], F32, name="wT")
            for n in range(2 * PASSES):
                nc.tensor.transpose(out=wT_of[i][:, n, :], in_=words[:, n * P : (n + 1) * P], identity=ident_f32[:])

        def regroup(i):
            if not 0 <= i < N_TILES:
                return
            first = unit_start(i)
            if i == first:
                count = 1 if ends_unit(i) else GROUP
                grouped_of[first] = mx_pool.tile([P, count, KEYS], BF16, name="grouped", align_bytes=64)
            nc.vector.tensor_copy(
                out=grouped_of[first][:, i - first, :].bitcast(F32).rearrange("p (g t u) -> p g t u", g=PASSES, u=2),
                in_=wT_of[i][:].rearrange("p (g u) t -> p g t u", g=PASSES),
            )

        def quantise(last):
            if not ends_unit(last):
                return
            first = unit_start(last)
            width = (last + 1 - first) * PASSES * P
            codes_of[first] = code_pool.tile([P, width], U32, name="codes", align_bytes=64)
            scales_of[first] = code_pool.tile([P, width], U8, name="scales", align_bytes=64)
            nc.vector.quantize_mx(
                out=codes_of[first][:].bitcast(FP8X4),
                scales=scales_of[first][:],
                in_=grouped_of[first][:].rearrange("p i k -> p (i k)"),
            )

        def gpsimd_after_quantise(last):
            if not ends_unit(last):
                return
            n = last // GROUP
            if EARLY_NORMS + n >= 2 * BATCHES and n + 1 >= BATCHES:
                return
            nc.gpsimd.tensor_copy(out=held[:, n : n + 1], in_=codes_of[unit_start(last)][:, 0:1])
            start_norms(EARLY_NORMS + n)
            regroup_v(n + 1)

        def weighted_sums(last):
            if not ends_unit(last):
                return
            first = unit_start(last)
            b = last // TILES_PER_BATCH
            if first >= N_TILES - SCALAR_DIVIDES:
                result_of[first] = score_psum.tile([P, last + 1 - first, C], F32, name="acc")
            else:
                result_of[first] = result_psum.tile([P, last + 1 - first, C], F32, name="result")
            for i in range(first, last + 1):
                for g in range(PASSES):
                    cols = slice(g * P, (g + 1) * P)
                    e_cols = slice(((i - first) * PASSES + g) * P, ((i - first) * PASSES + g + 1) * P)
                    nc.tensor.matmul_mx(
                        out=result_of[first][:, i - first, :],
                        lhsT=codes_of[first][:, e_cols].bitcast(FP8X4),
                        lhsT_scale=scales_of[first][:, e_cols],
                        rhs=v_codes[:, b, cols].bitcast(FP8X4),
                        rhs_scale=v_scales[:, b, cols],
                        start=(g == 0),
                        stop=(g == PASSES - 1),
                    )

        def invert_sums(last):
            if not ends_unit(last):
                return
            first = unit_start(last)
            if first < N_TILES - TILES_PER_BATCH:
                if first % TILES_PER_BATCH != 0:
                    return
                last = first + TILES_PER_BATCH - 1
            cols = slice(first, last + 1)
            nc.vector.reciprocal(out=inv_sum[:, cols], in_=row_sum[:, cols])

        def divide_and_store(last):
            if not ends_unit(last):
                return
            first = unit_start(last)
            count = last + 1 - first
            b, j = divmod(first, TILES_PER_BATCH)
            final = result_pool.tile([P, count, C], F32, name="final" if count == GROUP else "final_of_one")
            if first >= N_TILES - SCALAR_DIVIDES:
                for i in range(first, last + 1):
                    nc.scalar.activation(
                        out=final[:, i - first, :],
                        in_=result_of[first][:, i - first, :],
                        func=FUNC.Copy,
                        scale=inv_sum[:, i : i + 1],
                    )
            else:
                nc.vector.tensor_tensor(
                    out=final[:],
                    in0=result_of[first][:],
                    in1=inv_sum[:, first : last + 1].unsqueeze(2).to_broadcast([P, count, C]),
                    op=ALU.mult,
                )
            rows = out[b].rearrange("(p j) c -> p j c", j=TILES_PER_BATCH)
            nc.sync.dma_start(out=rows[:, j : j + count, :], in_=final[:])

        phase_ending_at = {}
        for n, count in enumerate(PHASES):
            phase_ending_at[sum(PHASES[: n + 1]) - 1] = (sum(PHASES[:n]), count)
        group_ending_at = {}
        for last_of_phase in phase_ending_at:
            first_of_phase, count = phase_ending_at[last_of_phase]
            end = last_of_phase
            for size in [1, 1, 2, 4] + ([4, 4] if first_of_phase == 0 else [8] * ((count - 8) // 8)):
                group_ending_at[end] = end - size + 1
                end -= size
            assert end == first_of_phase - 1
        for b in range(BATCHES):
            load_batch(b)
        make_identity(nc, ident_bf16[:])
        make_identity(nc, ident_f32[:])
        nc.vector.memset(one[:], 1.0)
        nc.scalar.activation(out=one_root[:], in_=one[:], func=FUNC.Sqrt)

        start_norms(0)
        start_norms(1)
        transpose_k(0)
        transpose_q(0)
        copy_k(0)
        copy_q(0)
        scores(0)
        pieces = [("norm", n) for n in range(2, 8)] + [("v", 0)] + [("norm", n) for n in range(8, EARLY_NORMS)]
        for r in range(N_TILES + LAG + 4):
            scores(r + 1)
            transpose_weights(r - LAG + 1)
            weighted_sums(r - LAG - 2)
            clamp_and_min(r)
            raise_q2(r)
            if r in group_ending_at:
                for i in range(group_ending_at[r], r + 1):
                    root(i)
            if r < len(pieces):
                kind, which = pieces[r]
                if kind == "norm":
                    start_norms(which)
                else:
                    regroup_v(which)
            b, step = divmod(r + NORMS_AHEAD, TILES_PER_BATCH)
            if 0 < b < BATCHES and step < 2:
                finish_norms(2 * b + step)
            b, step = divmod(r + PREPARE_AHEAD, TILES_PER_BATCH)
            if 0 < b < BATCHES:
                prepare(b, step)
            regroup(r - LAG)
            b, step = divmod(r - (LAG + GROUP), GROUP)
            if 0 <= b < BATCHES and step == 0:
                quantise_v(b)
            quantise(r - LAG - 1)
            gpsimd_after_quantise(r - LAG - 1)
            invert_sums(r - LAG - 2)
            divide_and_store(r - LAG - 3)
            if r in phase_ending_at:
                first, count = phase_ending_at[r]
                smallest_distances(first, count)
                for i in range(first, first + count):
                    weights(i)
